import numpy as np
import ml_dtypes


def mxq(x, axis, fmt="e4m3"):
    dtype, down = {"e4m3": (ml_dtypes.float8_e4m3fn, 7), "e5m2": (ml_dtypes.float8_e5m2, 14)}[fmt]
    v = np.moveaxis(np.asarray(x, np.float32).astype(ml_dtypes.bfloat16).astype(np.float64), axis, -1)
    blocks = v.reshape(v.shape[:-1] + (-1, 32))
    amax = np.abs(blocks).max(-1, keepdims=True)
    byte = np.maximum(np.where(amax > 0, np.frexp(amax)[1] - 1 + 127, 0) - down, 1)
    scale = np.exp2(byte - 127.0)
    codes = (blocks / scale).astype(np.float32).astype(dtype).astype(np.float64)
    return np.moveaxis((codes * scale).reshape(v.shape), -1, axis)


WIDE = False


def mx_kscale(k):
    if not WIDE:
        return np.ones(k)
    levels = np.array([10, -10, 5, -5, 0])
    a = np.random.permutation(np.resize(levels, k // 512 * 4)).reshape(k // 512, 4)
    idx = np.arange(k)
    return np.exp2(a[idx // 512, idx % 128 // 32])


BF16 = ml_dtypes.bfloat16


def bf(x):
    return np.asarray(x, np.float32).astype(BF16)


def f64(x):
    return np.asarray(x).astype(np.float64)


B, D_IN, H1, H2, H3, C = 8192, 2048, 2048, 2048, 1024, 512
BN_EPS = 1e-5


def bn_relu(z, gamma, beta):
    m = z.mean(axis=0)
    v = z.var(axis=0)
    return np.maximum((z - m) * (1.0 / np.sqrt(v + BN_EPS)) * gamma + beta, 0.0)


def setup_inputs():
    t = mx_kscale(H3)
    c = 32.0 * np.exp2(-15.0 * np.random.random(H3))
    mu = 0.5 * np.random.standard_normal(H3)
    return {"z2": bf((np.random.standard_normal((B, H3)) + mu) * c),
            "g2": bf((1.0 + 0.1 * np.random.standard_normal(H3)) * t),
            "beta2": bf(0.2 * np.random.standard_normal(H3) * t),
            "W3": bf(np.random.standard_normal((C, H3)) * 3.0 / np.sqrt(H3) / t),
            "b3": bf(0.5 * np.random.standard_normal(C))}


def reference(z2, g2, beta2, W3, b3):
    h = bn_relu(f64(z2), f64(g2), f64(beta2))
    logits = (mxq(h, 1, "e4m3") @ mxq(f64(W3), 1, "e4m3").T) + f64(b3)
    s = logits - logits.max(axis=1, keepdims=True)
    return s - np.log(np.exp(s).sum(axis=1, keepdims=True))

@@ -1,0 +1,303 @@
+from contextlib import ExitStack
+
+import concourse.mybir as mybir
+from concourse.masks import make_identity
+
+F32 = mybir.dt.float32
+BF16 = mybir.dt.bfloat16
+U32 = mybir.dt.uint32
+U8 = mybir.dt.uint8
+FP8X4 = mybir.dt.float8_e4m3fn_x4
+ALU = mybir.AluOpType
+ACT = mybir.ActivationFunctionType
+AX = mybir.AxisListType
+
+P = 128
+B = 8192
+K = 1024
+C = 512
+KT = K // P
+G = 8
+GB = B // G
+U = 16
+UB = B // U
+JH = UB // P
+J = GB // P
+NG = 3
+BN_EPS = 1e-5
+ROOT = 1024.0
+AFF_V = (0, 1, 2, 3, 4, 5, 6, 7)
+R_V = ((0, 0),)
+E4_V = ()
+
+FLOPS = 2 * B * K * C
+
+
+def tile_binarymlp_pb_t_kernel(tc, z2, g2, beta2, W3, b3, out):
+    nc = tc.nc
+    with ExitStack() as ctx:
+        const = ctx.enter_context(tc.tile_pool(name="const", bufs=1))
+        ztp = ctx.enter_context(tc.tile_pool(name="ztp", bufs=1))
+        stream = ctx.enter_context(tc.tile_pool(name="stream", bufs=5))
+        grp = ctx.enter_context(tc.tile_pool(name="grp", bufs=2))
+        cod = ctx.enter_context(tc.tile_pool(name="cod", bufs=4))
+        small = ctx.enter_context(tc.tile_pool(name="small", bufs=3))
+        psum = ctx.enter_context(tc.psum_pool(name="psum", bufs=5))
+        gpsum = ctx.enter_context(tc.psum_pool(name="gpsum", bufs=1))
+
+        one = const.tile([P, 1], F32, name="one")
+        nc.vector.memset(one[:], 1.0)
+        warm = const.tile([P, 1], F32, name="warm")
+        nc.scalar.activation(out=warm[:], in_=one[:], func=ACT.Sqrt)
+
+        ident = const.tile([P, P], BF16, name="ident")
+        make_identity(nc, ident[:])
+        ones = const.tile([P, P], BF16, name="ones")
+        nc.vector.memset(ones[:], 1.0)
+        brow = const.tile([P, C], BF16, name="brow")
+        nc.vector.memset(brow[:], 0.0)
+        vecs = const.tile([P, P], BF16, name="vecs")
+        nc.vector.memset(vecs[:], 0.0)
+        nc.gpsimd.dma_start(out=brow[0:1, :], in_=b3.rearrange("(o c) -> o c", o=1))
+        nc.gpsimd.dma_start(out=vecs[0:KT, :], in_=g2.rearrange("(t p) -> t p", p=P))
+        nc.gpsimd.dma_start(out=vecs[KT : 2 * KT, :], in_=beta2.rearrange("(t p) -> t p", p=P))
+        wn = const.tile([P, C // P, K], BF16, name="wn")
+        nc.gpsimd.dma_start(out=wn[:], in_=W3.rearrange("(t p) k -> p t k", p=P))
+
+        pv = psum.tile([P, P], BF16, tag="ps", name="pv")
+        nc.tensor.transpose(pv[:], vecs[:], ident[:])
+        gb = const.tile([P, 2 * KT], F32, name="gb")
+        nc.vector.tensor_copy(out=gb[:], in_=pv[:, 0 : 2 * KT])
+        pb = psum.tile([P, C], F32, tag="ps", name="pb")
+        nc.tensor.matmul(out=pb[:], lhsT=ones[:], rhs=brow[:], start=True, stop=True)
+        bias_bc = const.tile([P, C], F32, name="bias_bc")
+        nc.vector.tensor_copy(out=bias_bc[:], in_=pb[:])
+
+        zts = []
+        for g in range(G):
+            zts.append(ztp.tile([P, KT, GB], BF16, name="zt%d" % g))
+        s1 = const.tile([P, KT, U], F32, name="s1")
+        sq = const.tile([P, KT, G], F32, name="sq")
+        junk_s = const.tile([P, GB], BF16, name="junk_s")
+        junk_e = const.tile([P, C], BF16, name="junk_e")
+        junk_d = const.tile([P, P], F32, name="junk_d")
+        grams = []
+        for i in range(NG):
+            grams.append(gpsum.tile([P, P], F32, name="gram%d" % i))
+
+        for u in range(U):
+            g, h = divmod(u, 2)
+            zn = stream.tile([P, JH, K], BF16, tag="st", name="zn")
+            nc.sync.dma_start(
+                out=zn[:],
+                in_=z2[u * UB : (u + 1) * UB, :].rearrange("(p j) k -> p j k", j=JH),
+            )
+            for kt in range(KT):
+                ks = slice(kt * P, (kt + 1) * P)
+                pt = psum.tile([P, UB], BF16, tag="ps", name="pt")
+                for j in range(JH):
+                    nc.tensor.transpose(pt[:, j * P : (j + 1) * P], zn[:, j, ks], ident[:])
+                if kt < NG:
+                    for j in range(JH):
+                        nc.tensor.matmul(
+                            out=grams[kt][:],
+                            lhsT=zn[:, j, ks],
+                            rhs=zn[:, j, ks],
+                            start=(u == 0 and j == 0),
+                            stop=(u == U - 1 and j == JH - 1),
+                        )
+                nc.vector.tensor_scalar(
+                    out=zts[g][:, kt, h * UB : (h + 1) * UB],
+                    in0=pt[:],
+                    scalar1=1.0,
+                    scalar2=None,
+                    op0=ALU.mult,
+                    op1=ALU.add,
+                    accum_out=s1[:, kt, u : u + 1],
+                )
+                if h == 1 and kt >= NG:
+                    nc.scalar.activation(
+                        out=junk_s[:],
+                        in_=zts[g][:, kt, :],
+                        func=ACT.Square,
+                        accum_out=sq[:, kt, g : g + 1],
+                    )
+
+        wt = stream.tile([P, KT, C], BF16, tag="st", name="wt")
+        for kt in range(KT):
+            ks = slice(kt * P, (kt + 1) * P)
+            pw = psum.tile([P, C], BF16, tag="ps", name="pw")
+            for t in range(C // P):
+                nc.tensor.transpose(pw[:, t * P : (t + 1) * P], wn[:, t, ks], ident[:])
+            nc.scalar.copy(out=wt[:, kt, :], in_=pw[:])
+        gw = grp.tile([P, 2, C, 4], BF16, tag="gr", name="gw", align_bytes=64)
+        nc.vector.tensor_copy(out=gw[:], in_=wt[:].rearrange("p (c t) n -> p c n t", t=4))
+        wcodes = const.tile([P, 2 * C], U32, name="wcodes", align_bytes=64)
+        wscl = const.tile([P, 2 * C], U8, name="wscl", align_bytes=64)
+        nc.vector.quantize_mx(
+            out=wcodes[:].bitcast(FP8X4),
+            scales=wscl[:],
+            in_=gw[:].rearrange("p c n t -> p (c n t)"),
+        )
+
+        ssum = const.tile([P, KT], F32, name="ssum")
+        nc.vector.tensor_reduce(out=ssum[:], in_=s1[:], axis=AX.X, op=ALU.add)
+        ssq = const.tile([P, KT], F32, name="ssq")
+        nc.vector.tensor_reduce(out=ssq[:, NG:KT], in_=sq[:, NG:KT, :], axis=AX.X, op=ALU.add)
+        for i in range(NG):
+            nc.vector.scalar_tensor_tensor(
+                out=junk_d[:],
+                in0=grams[i][:],
+                scalar=1.0,
+                in1=ident[:],
+                op0=ALU.mult,
+                op1=ALU.mult,
+                accum_out=ssq[:, i : i + 1],
+            )
+        mean = const.tile([P, KT], F32, name="mean")
+        nc.vector.tensor_scalar(out=mean[:], in0=ssum[:], scalar1=1.0 / B, scalar2=None, op0=ALU.mult)
+        m2 = const.tile([P, KT], F32, name="m2")
+        nc.vector.tensor_tensor(out=m2[:], in0=mean[:], in1=mean[:], op=ALU.mult)
+        var = const.tile([P, KT], F32, name="var")
+        nc.vector.scalar_tensor_tensor(
+            out=var[:], in0=ssq[:], scalar=1.0 / B, in1=m2[:], op0=ALU.mult, op1=ALU.subtract
+        )
+        ve = const.tile([P, KT], F32, name="ve")
+        nc.vector.tensor_scalar(
+            out=ve[:], in0=var[:], scalar1=0.0, scalar2=BN_EPS, op0=ALU.max, op1=ALU.add
+        )
+        sd = const.tile([P, KT], F32, name="sd")
+        nc.scalar.activation(out=sd[:], in_=ve[:], func=ACT.Sqrt)
+        rstd = const.tile([P, KT], F32, name="rstd")
+        nc.vector.reciprocal(out=rstd[:], in_=sd[:])
+        a = const.tile([P, KT], F32, name="a")
+        nc.vector.tensor_tensor(out=a[:], in0=gb[:, 0:KT], in1=rstd[:], op=ALU.mult)
+        ma = const.tile([P, KT], F32, name="ma")
+        nc.vector.tensor_tensor(out=ma[:], in0=mean[:], in1=a[:], op=ALU.mult)
+        bb = const.tile([P, KT], F32, name="bb")
+        nc.vector.tensor_tensor(out=bb[:], in0=gb[:, KT : 2 * KT], in1=ma[:], op=ALU.subtract)
+
+        pe_pos = const.tile([P, J], F32, name="pe_pos")
+        nc.gpsimd.memset(pe_pos[:], 1.0 / ROOT)
+        pe_neg = const.tile([P, J], F32, name="pe_neg")
+        nc.gpsimd.memset(pe_neg[:], -1.0 / ROOT)
+
+        for g in range(G):
+            zt = zts[g]
+            for kt in range(KT):
+                if kt in AFF_V:
+                    nc.vector.tensor_scalar(
+                        out=zt[:, kt, :],
+                        in0=zt[:, kt, :],
+                        scalar1=a[:, kt : kt + 1],
+                        scalar2=bb[:, kt : kt + 1],
+                        op0=ALU.mult,
+                        op1=ALU.add,
+                    )
+                else:
+                    nc.scalar.activation(
+                        out=zt[:, kt, :],
+                        in_=zt[:, kt, :],
+                        func=ACT.Relu,
+                        bias=bb[:, kt : kt + 1],
+                        scale=a[:, kt : kt + 1],
+                    )
+
+            neg_m = small.tile([P, J], F32, name="neg_m")
+            esum = small.tile([P, J], F32, name="esum")
+            ls = []
+            for h in range(2):
+                gh = grp.tile([P, 2, UB, 4], BF16, tag="gr", name="gh", align_bytes=64)
+                for c in range(2):
+                    dst = gh[:, c, :, :].rearrange("p (n i) t -> p n t i", i=4)
+                    src = zt[:, 4 * c : 4 * c + 4, h * UB : (h + 1) * UB].rearrange(
+                        "p t (n i) -> p n t i", i=4
+                    )
+                    if (h, c) in R_V:
+                        nc.vector.tensor_scalar(
+                            out=dst, in0=src, scalar1=0.0, scalar2=None, op0=ALU.max
+                        )
+                    else:
+                        nc.scalar.activation(out=dst, in_=src, func=ACT.Relu)
+                cd = cod.tile([P, 2 * UB], U32, tag="cd", name="cd", align_bytes=64)
+                sc = cod.tile([P, 2 * UB], U8, tag="sc", name="sc", align_bytes=64)
+                nc.vector.quantize_mx(
+                    out=cd[:].bitcast(FP8X4),
+                    scales=sc[:],
+                    in_=gh[:].rearrange("p c b t -> p (c b t)"),
+                )
+
+                lt = stream.tile([P, JH, C], F32, tag="st", name="lt")
+                ls.append(lt)
+                for jj in range(JH):
+                    acc = psum.tile([P, C], F32, tag="ps", name="acc")
+                    for c in range(2):
+                        col = c * UB + jj * P
+                        nc.tensor.matmul_mx(
+                            out=acc[:],
+                            lhsT=cd[:, col : col + P].bitcast(FP8X4),
+                            lhsT_scale=sc[:, col : col + P],
+                            rhs=wcodes[:, c * C : (c + 1) * C].bitcast(FP8X4),
+                            rhs_scale=wscl[:, c * C : (c + 1) * C],
+                            start=(c == 0),
+                            stop=(c == 1),
+                        )
+                    nc.vector.tensor_tensor(out=lt[:, jj, :], in0=acc[:], in1=bias_bc[:], op=ALU.add)
+                nc.vector.tensor_reduce(
+                    out=neg_m[:, h * JH : (h + 1) * JH], in_=lt[:], axis=AX.X, op=ALU.max, negate=True
+                )
+                for jj in range(JH):
+                    j = h * JH + jj
+                    nc.scalar.activation(
+                        out=junk_e[:],
+                        in_=lt[:, jj, :],
+                        func=ACT.Exp,
+                        bias=neg_m[:, j : j + 1],
+                        scale=1.0,
+                        accum_out=esum[:, j : j + 1],
+                    )
+
+            r_pos = small.tile([P, J], F32, name="r_pos")
+            nc.gpsimd.tensor_tensor(out=r_pos[:], in0=esum[:], in1=pe_pos[:], op=ALU.pow)
+            r_neg = small.tile([P, J], F32, name="r_neg")
+            nc.gpsimd.tensor_tensor(out=r_neg[:], in0=esum[:], in1=pe_neg[:], op=ALU.pow)
+            t = small.tile([P, J], F32, name="t")
+            nc.gpsimd.tensor_tensor(out=t[:], in0=r_pos[:], in1=r_neg[:], op=ALU.subtract)
+            e = small.tile([P, J], F32, name="e")
+            nc.scalar.activation(out=e[:], in_=t[:], func=ACT.Exp, scale=-0.5 * ROOT)
+            q = small.tile([P, J], F32, name="q")
+            nc.gpsimd.tensor_scalar(
+                out=q[:], in0=t[:], scalar1=-0.5 * ROOT, scalar2=1.0, op0=ALU.mult, op1=ALU.add
+            )
+            q2 = small.tile([P, J], F32, name="q2")
+            nc.gpsimd.tensor_tensor(out=q2[:], in0=q[:], in1=neg_m[:], op=ALU.add)
+            w = small.tile([P, J], F32, name="w")
+            nc.gpsimd.tensor_tensor(out=w[:], in0=esum[:], in1=e[:], op=ALU.mult)
+            neg_c = small.tile([P, J], F32, name="neg_c")
+            nc.gpsimd.tensor_tensor(out=neg_c[:], in0=q2[:], in1=w[:], op=ALU.subtract)
+
+            for h in range(2):
+                lt = ls[h]
+                u = 2 * g + h
+                for jj in range(JH):
+                    j = h * JH + jj
+                    if j in E4_V:
+                        nc.vector.tensor_scalar(
+                            out=lt[:, jj, :],
+                            in0=lt[:, jj, :],
+                            scalar1=neg_c[:, j : j + 1],
+                            scalar2=None,
+                            op0=ALU.add,
+                        )
+                    else:
+                        nc.scalar.activation(
+                            out=lt[:, jj, :],
+                            in_=lt[:, jj, :],
+                            func=ACT.Identity,
+                            bias=neg_c[:, j : j + 1],
+                            scale=1.0,
+                        )
+                nc.sync.dma_start(
+                    out=out[u * UB : (u + 1) * UB, :].rearrange("(p j) c -> p j c", j=JH),
+                    in_=lt[:],
+                )

@@ -7,6 +7,7 @@ F32 = mybir.dt.float32
 BF16 = mybir.dt.bfloat16
 U32 = mybir.dt.uint32
 U8 = mybir.dt.uint8
+I32 = mybir.dt.int32
 FP8X4 = mybir.dt.float8_e4m3fn_x4
 ALU = mybir.AluOpType
 ACT = mybir.ActivationFunctionType
@@ -24,11 +25,12 @@ UB = B // U
 JH = UB // P
 J = GB // P
 NG = 3
+KS = KT - NG
 BN_EPS = 1e-5
 ROOT = 1024.0
-AFF_V = (0, 1, 2, 3, 4, 5, 6, 7)
-R_V = ((0, 0),)
-E4_V = ()
+N_WARM = 12
+R_V = ((0, 0), (1, 1), (3, 0))
+U_QW = 4
 
 FLOPS = 2 * B * K * C
 
@@ -37,18 +39,33 @@ def tile_binarymlp_pb_t_kernel(tc, z2, g2, beta2, W3, b3, out):
     nc = tc.nc
     with ExitStack() as ctx:
         const = ctx.enter_context(tc.tile_pool(name="const", bufs=1))
-        ztp = ctx.enter_context(tc.tile_pool(name="ztp", bufs=1))
-        stream = ctx.enter_context(tc.tile_pool(name="stream", bufs=5))
+        big = ctx.enter_context(tc.tile_pool(name="big", bufs=11))
         grp = ctx.enter_context(tc.tile_pool(name="grp", bufs=2))
         cod = ctx.enter_context(tc.tile_pool(name="cod", bufs=4))
-        small = ctx.enter_context(tc.tile_pool(name="small", bufs=3))
-        psum = ctx.enter_context(tc.psum_pool(name="psum", bufs=5))
-        gpsum = ctx.enter_context(tc.psum_pool(name="gpsum", bufs=1))
+        small = ctx.enter_context(tc.tile_pool(name="small", bufs=4))
+        psum = ctx.enter_context(tc.psum_pool(name="psum", bufs=8))
+        ctx.enter_context(tc.manual_schedule())
 
+        wcodes = const.tile([P, 2 * C], U32, name="wcodes", align_bytes=64)
+        wscl = const.tile([P, 2 * C], U8, name="wscl", align_bytes=64)
+        nc.vector.memset(wcodes[:, 0:C].bitcast(I32), 0)
+        nc.vector.memset(wscl[:, 0:C].bitcast(I32), 0)
         one = const.tile([P, 1], F32, name="one")
         nc.vector.memset(one[:], 1.0)
         warm = const.tile([P, 1], F32, name="warm")
         nc.scalar.activation(out=warm[:], in_=one[:], func=ACT.Sqrt)
+
+        pwarm = psum.tile([P, C], F32, tag="ps", name="pwarm")
+        for i in range(N_WARM):
+            nc.tensor.matmul_mx(
+                out=pwarm[:],
+                lhsT=wcodes[:, 0:P].bitcast(FP8X4),
+                lhsT_scale=wscl[:, 0:P],
+                rhs=wcodes[:, 0:C].bitcast(FP8X4),
+                rhs_scale=wscl[:, 0:C],
+                start=True,
+                stop=True,
+            )
 
         ident = const.tile([P, P], BF16, name="ident")
         make_identity(nc, ident[:])
@@ -61,53 +78,55 @@ def tile_binarymlp_pb_t_kernel(tc, z2, g2, beta2, W3, b3, out):
         nc.gpsimd.dma_start(out=brow[0:1, :], in_=b3.rearrange("(o c) -> o c", o=1))
         nc.gpsimd.dma_start(out=vecs[0:KT, :], in_=g2.rearrange("(t p) -> t p", p=P))
         nc.gpsimd.dma_start(out=vecs[KT : 2 * KT, :], in_=beta2.rearrange("(t p) -> t p", p=P))
-        wn = const.tile([P, C // P, K], BF16, name="wn")
-        nc.gpsimd.dma_start(out=wn[:], in_=W3.rearrange("(t p) k -> p t k", p=P))
+        pe_pos = const.tile([P, J], F32, name="pe_pos")
+        nc.gpsimd.memset(pe_pos[:], 1.0 / ROOT)
+        pe_neg = const.tile([P, J], F32, name="pe_neg")
+        nc.gpsimd.memset(pe_neg[:], -1.0 / ROOT)
 
-        pv = psum.tile([P, P], BF16, tag="ps", name="pv")
-        nc.tensor.transpose(pv[:], vecs[:], ident[:])
-        gb = const.tile([P, 2 * KT], F32, name="gb")
-        nc.vector.tensor_copy(out=gb[:], in_=pv[:, 0 : 2 * KT])
-        pb = psum.tile([P, C], F32, tag="ps", name="pb")
-        nc.tensor.matmul(out=pb[:], lhsT=ones[:], rhs=brow[:], start=True, stop=True)
-        bias_bc = const.tile([P, C], F32, name="bias_bc")
-        nc.vector.tensor_copy(out=bias_bc[:], in_=pb[:])
-
-        zts = []
-        for g in range(G):
-            zts.append(ztp.tile([P, KT, GB], BF16, name="zt%d" % g))
         s1 = const.tile([P, KT, U], F32, name="s1")
-        sq = const.tile([P, KT, G], F32, name="sq")
+        sq = const.tile([P, KS, G + 1], F32, name="sq")
+        ssq = const.tile([P, KT], F32, name="ssq")
         junk_s = const.tile([P, GB], BF16, name="junk_s")
         junk_e = const.tile([P, C], BF16, name="junk_e")
         junk_d = const.tile([P, P], F32, name="junk_d")
+        gb = const.tile([P, 2 * KT], F32, name="gb")
+        bias_bc = const.tile([P, C], F32, name="bias_bc")
         grams = []
         for i in range(NG):
-            grams.append(gpsum.tile([P, P], F32, name="gram%d" % i))
+            grams.append(psum.tile([P, P], F32, tag="ps", name="gram%d" % i))
 
+        zts = []
+        gw = None
         for u in range(U):
             g, h = divmod(u, 2)
-            zn = stream.tile([P, JH, K], BF16, tag="st", name="zn")
+            if h == 0:
+                zts.append(big.tile([P, KT, GB], BF16, tag="big", name="zt%d" % g))
+            zt = zts[g]
+            zn = big.tile([P, JH, K], BF16, tag="big", name="zn")
             nc.sync.dma_start(
                 out=zn[:],
                 in_=z2[u * UB : (u + 1) * UB, :].rearrange("(p j) k -> p j k", j=JH),
             )
+            if u == 0:
+                wn = big.tile([P, C // P, K], BF16, tag="big", name="wn")
+                nc.sync.dma_start(out=wn[:], in_=W3.rearrange("(t p) k -> p t k", p=P))
+            for i in range(NG):
+                ks = slice((KS + i) * P, (KS + i + 1) * P)
+                for jj in range(JH):
+                    nc.tensor.matmul(
+                        out=grams[i][:],
+                        lhsT=zn[:, jj, ks],
+                        rhs=zn[:, jj, ks],
+                        start=(u == 0 and jj == 0),
+                        stop=(u == U - 1 and jj == JH - 1),
+                    )
             for kt in range(KT):
                 ks = slice(kt * P, (kt + 1) * P)
                 pt = psum.tile([P, UB], BF16, tag="ps", name="pt")
-                for j in range(JH):
-                    nc.tensor.transpose(pt[:, j * P : (j + 1) * P], zn[:, j, ks], ident[:])
-                if kt < NG:
-                    for j in range(JH):
-                        nc.tensor.matmul(
-                            out=grams[kt][:],
-                            lhsT=zn[:, j, ks],
-                            rhs=zn[:, j, ks],
-                            start=(u == 0 and j == 0),
-                            stop=(u == U - 1 and j == JH - 1),
-                        )
+                for jj in range(JH):
+                    nc.tensor.transpose(pt[:, jj * P : (jj + 1) * P], zn[:, jj, ks], ident[:])
                 nc.vector.tensor_scalar(
-                    out=zts[g][:, kt, h * UB : (h + 1) * UB],
+                    out=zt[:, kt, h * UB : (h + 1) * UB],
                     in0=pt[:],
                     scalar1=1.0,
                     scalar2=None,
@@ -115,49 +134,70 @@ def tile_binarymlp_pb_t_kernel(tc, z2, g2, beta2, W3, b3, out):
                     op1=ALU.add,
                     accum_out=s1[:, kt, u : u + 1],
                 )
-                if h == 1 and kt >= NG:
-                    nc.scalar.activation(
-                        out=junk_s[:],
-                        in_=zts[g][:, kt, :],
-                        func=ACT.Square,
-                        accum_out=sq[:, kt, g : g + 1],
-                    )
+                if kt < KS:
+                    if g == G - 1:
+                        nc.scalar.activation(
+                            out=junk_s[:, 0:UB],
+                            in_=zt[:, kt, h * UB : (h + 1) * UB],
+                            func=ACT.Square,
+                            accum_out=sq[:, kt, g + h : g + h + 1],
+                        )
+                    elif h == 1:
+                        nc.scalar.activation(
+                            out=junk_s[:],
+                            in_=zt[:, kt, :],
+                            func=ACT.Square,
+                            accum_out=sq[:, kt, g : g + 1],
+                        )
+                if u == U - 1 and kt == 1:
+                    for i in range(NG):
+                        nc.vector.scalar_tensor_tensor(
+                            out=junk_d[:],
+                            in0=grams[i][:],
+                            scalar=1.0,
+                            in1=ident[:],
+                            op0=ALU.mult,
+                            op1=ALU.mult,
+                            accum_out=ssq[:, KS + i : KS + i + 1],
+                        )
 
-        wt = stream.tile([P, KT, C], BF16, tag="st", name="wt")
-        for kt in range(KT):
-            ks = slice(kt * P, (kt + 1) * P)
-            pw = psum.tile([P, C], BF16, tag="ps", name="pw")
-            for t in range(C // P):
-                nc.tensor.transpose(pw[:, t * P : (t + 1) * P], wn[:, t, ks], ident[:])
-            nc.scalar.copy(out=wt[:, kt, :], in_=pw[:])
-        gw = grp.tile([P, 2, C, 4], BF16, tag="gr", name="gw", align_bytes=64)
-        nc.vector.tensor_copy(out=gw[:], in_=wt[:].rearrange("p (c t) n -> p c n t", t=4))
-        wcodes = const.tile([P, 2 * C], U32, name="wcodes", align_bytes=64)
-        wscl = const.tile([P, 2 * C], U8, name="wscl", align_bytes=64)
-        nc.vector.quantize_mx(
-            out=wcodes[:].bitcast(FP8X4),
-            scales=wscl[:],
-            in_=gw[:].rearrange("p c n t -> p (c n t)"),
-        )
+            if u == 0:
+                pv = psum.tile([P, P], BF16, tag="ps", name="pv")
+                nc.tensor.transpose(pv[:], vecs[:], ident[:])
+                nc.vector.tensor_copy(out=gb[:], in_=pv[:, 0 : 2 * KT])
+                pb = psum.tile([P, C], F32, tag="ps", name="pb")
+                nc.tensor.matmul(out=pb[:], lhsT=ones[:], rhs=brow[:], start=True, stop=True)
+                nc.scalar.copy(out=bias_bc[:], in_=pb[:])
+                wt = big.tile([P, KT, C], BF16, tag="big", name="wt")
+                for kt in range(KT):
+                    ks = slice(kt * P, (kt + 1) * P)
+                    pw = psum.tile([P, C], BF16, tag="ps", name="pw")
+                    for t in range(C // P):
+                        nc.tensor.transpose(pw[:, t * P : (t + 1) * P], wn[:, t, ks], ident[:])
+                    nc.scalar.copy(out=wt[:, kt, :], in_=pw[:])
+                gw = grp.tile([P, 2, C, 4], BF16, tag="gr", name="gw", align_bytes=64)
+                nc.gpsimd.tensor_scalar(
+                    out=gw[:],
+                    in0=wt[:].rearrange("p (c t) n -> p c n t", t=4),
+                    scalar1=1.0,
+                    scalar2=0.0,
+                    op0=ALU.mult,
+                    op1=ALU.add,
+                )
+            if u == U_QW:
+                nc.vector.quantize_mx(
+                    out=wcodes[:].bitcast(FP8X4),
+                    scales=wscl[:],
+                    in_=gw[:].rearrange("p c n t -> p (c n t)"),
+                )
 
         ssum = const.tile([P, KT], F32, name="ssum")
         nc.vector.tensor_reduce(out=ssum[:], in_=s1[:], axis=AX.X, op=ALU.add)
-        ssq = const.tile([P, KT], F32, name="ssq")
-        nc.vector.tensor_reduce(out=ssq[:, NG:KT], in_=sq[:, NG:KT, :], axis=AX.X, op=ALU.add)
-        for i in range(NG):
-            nc.vector.scalar_tensor_tensor(
-                out=junk_d[:],
-                in0=grams[i][:],
-                scalar=1.0,
-                in1=ident[:],
-                op0=ALU.mult,
-                op1=ALU.mult,
-                accum_out=ssq[:, i : i + 1],
-            )
-        mean = const.tile([P, KT], F32, name="mean")
-        nc.vector.tensor_scalar(out=mean[:], in0=ssum[:], scalar1=1.0 / B, scalar2=None, op0=ALU.mult)
+        nc.vector.tensor_reduce(out=ssq[:, 0:KS], in_=sq[:], axis=AX.X, op=ALU.add)
         m2 = const.tile([P, KT], F32, name="m2")
-        nc.vector.tensor_tensor(out=m2[:], in0=mean[:], in1=mean[:], op=ALU.mult)
+        nc.vector.scalar_tensor_tensor(
+            out=m2[:], in0=ssum[:], scalar=1.0 / (B * B), in1=ssum[:], op0=ALU.mult, op1=ALU.mult
+        )
         var = const.tile([P, KT], F32, name="var")
         nc.vector.scalar_tensor_tensor(
             out=var[:], in0=ssq[:], scalar=1.0 / B, in1=m2[:], op0=ALU.mult, op1=ALU.subtract
@@ -168,6 +208,8 @@ def tile_binarymlp_pb_t_kernel(tc, z2, g2, beta2, W3, b3, out):
         )
         sd = const.tile([P, KT], F32, name="sd")
         nc.scalar.activation(out=sd[:], in_=ve[:], func=ACT.Sqrt)
+        mean = const.tile([P, KT], F32, name="mean")
+        nc.vector.tensor_scalar(out=mean[:], in0=ssum[:], scalar1=1.0 / B, scalar2=None, op0=ALU.mult)
         rstd = const.tile([P, KT], F32, name="rstd")
         nc.vector.reciprocal(out=rstd[:], in_=sd[:])
         a = const.tile([P, KT], F32, name="a")
@@ -177,127 +219,214 @@ def tile_binarymlp_pb_t_kernel(tc, z2, g2, beta2, W3, b3, out):
         bb = const.tile([P, KT], F32, name="bb")
         nc.vector.tensor_tensor(out=bb[:], in0=gb[:, KT : 2 * KT], in1=ma[:], op=ALU.subtract)
 
-        pe_pos = const.tile([P, J], F32, name="pe_pos")
-        nc.gpsimd.memset(pe_pos[:], 1.0 / ROOT)
-        pe_neg = const.tile([P, J], F32, name="pe_neg")
-        nc.gpsimd.memset(pe_neg[:], -1.0 / ROOT)
+        ghs = {}
+        cds = {}
+        scs = {}
+        accs = {}
+        lts = {}
+        negs = {}
+        esums = {}
+        lnt = {}
+        lne = {}
+        lnq = {}
+        shifts = {}
 
-        for g in range(G):
-            zt = zts[g]
-            for kt in range(KT):
-                if kt in AFF_V:
+        def affine(g, kts):
+            for kt in kts:
+                nc.vector.tensor_scalar(
+                    out=zts[g][:, kt, :],
+                    in0=zts[g][:, kt, :],
+                    scalar1=a[:, kt : kt + 1],
+                    scalar2=bb[:, kt : kt + 1],
+                    op0=ALU.mult,
+                    op1=ALU.add,
+                )
+
+        def regroup(u):
+            g, h = divmod(u, 2)
+            gh = grp.tile([P, 2, UB, 4], BF16, tag="gr", name="gh", align_bytes=64)
+            ghs[u] = gh
+            for c in range(2):
+                dst = gh[:, c, :, :].rearrange("p (n i) t -> p n t i", i=4)
+                src = zts[g][:, 4 * c : 4 * c + 4, h * UB : (h + 1) * UB].rearrange(
+                    "p t (n i) -> p n t i", i=4
+                )
+                if (u % 4, c) in R_V:
+                    nc.vector.tensor_scalar(out=dst, in0=src, scalar1=0.0, scalar2=None, op0=ALU.max)
+                else:
+                    nc.scalar.activation(out=dst, in_=src, func=ACT.Relu)
+
+        def quant(u):
+            cd = cod.tile([P, 2 * UB], U32, tag="cd", name="cd", align_bytes=64)
+            sc = cod.tile([P, 2 * UB], U8, tag="sc", name="sc", align_bytes=64)
+            cds[u] = cd
+            scs[u] = sc
+            nc.vector.quantize_mx(
+                out=cd[:].bitcast(FP8X4),
+                scales=sc[:],
+                in_=ghs[u][:].rearrange("p c b t -> p (c b t)"),
+            )
+
+        def mx(u):
+            for jj in range(JH):
+                acc = psum.tile([P, C], F32, tag="ps", name="acc")
+                accs[(u, jj)] = acc
+                for c in range(2):
+                    col = c * UB + jj * P
+                    nc.tensor.matmul_mx(
+                        out=acc[:],
+                        lhsT=cds[u][:, col : col + P].bitcast(FP8X4),
+                        lhsT_scale=scs[u][:, col : col + P],
+                        rhs=wcodes[:, c * C : (c + 1) * C].bitcast(FP8X4),
+                        rhs_scale=wscl[:, c * C : (c + 1) * C],
+                        start=(c == 0),
+                        stop=(c == 1),
+                    )
+
+        def bias_max(u):
+            g, h = divmod(u, 2)
+            if h == 0:
+                lts[g] = big.tile([P, J, C], F32, tag="big", name="lt")
+                negs[g] = small.tile([P, J], F32, name="neg_m")
+                esums[g] = small.tile([P, J], F32, name="esum")
+            lt = lts[g]
+            for jj in range(JH):
+                nc.vector.tensor_tensor(
+                    out=lt[:, h * JH + jj, :], in0=accs[(u, jj)][:], in1=bias_bc[:], op=ALU.add
+                )
+            nc.vector.tensor_reduce(
+                out=negs[g][:, h * JH : (h + 1) * JH],
+                in_=lt[:, h * JH : (h + 1) * JH, :],
+                axis=AX.X,
+                op=ALU.max,
+                negate=True,
+            )
+
+        def expsum(u):
+            g, h = divmod(u, 2)
+            for jj in range(JH):
+                j = h * JH + jj
+                nc.scalar.activation(
+                    out=junk_e[:],
+                    in_=lts[g][:, j, :],
+                    func=ACT.Exp,
+                    bias=negs[g][:, j : j + 1],
+                    scale=1.0,
+                    accum_out=esums[g][:, j : j + 1],
+                )
+
+        def ln_guess(g, j0, j1):
+            n = j1 - j0
+            r_pos = small.tile([P, J], F32, name="r_pos")
+            nc.gpsimd.tensor_tensor(
+                out=r_pos[:, 0:n], in0=esums[g][:, j0:j1], in1=pe_pos[:, 0:n], op=ALU.pow
+            )
+            r_neg = small.tile([P, J], F32, name="r_neg")
+            nc.gpsimd.tensor_tensor(
+                out=r_neg[:, 0:n], in0=esums[g][:, j0:j1], in1=pe_neg[:, 0:n], op=ALU.pow
+            )
+            t = small.tile([P, J], F32, name="t")
+            lnt[(g, j0)] = t
+            nc.gpsimd.tensor_tensor(
+                out=t[:, 0:n], in0=r_pos[:, 0:n], in1=r_neg[:, 0:n], op=ALU.subtract
+            )
+            q = small.tile([P, J], F32, name="q")
+            nc.gpsimd.tensor_scalar(
+                out=q[:, 0:n],
+                in0=t[:, 0:n],
+                scalar1=-0.5 * ROOT,
+                scalar2=1.0,
+                op0=ALU.mult,
+                op1=ALU.add,
+            )
+            q2 = small.tile([P, J], F32, name="q2")
+            lnq[(g, j0)] = q2
+            nc.gpsimd.tensor_tensor(
+                out=q2[:, 0:n], in0=q[:, 0:n], in1=negs[g][:, j0:j1], op=ALU.add
+            )
+
+        def ln_step(g, j0, j1):
+            n = j1 - j0
+            e = small.tile([P, J], F32, name="e")
+            nc.scalar.activation(
+                out=e[:, 0:n], in_=lnt[(g, j0)][:, 0:n], func=ACT.Exp, scale=-0.5 * ROOT
+            )
+            w = small.tile([P, J], F32, name="w")
+            nc.gpsimd.tensor_tensor(
+                out=w[:, 0:n], in0=esums[g][:, j0:j1], in1=e[:, 0:n], op=ALU.mult
+            )
+            neg_c = small.tile([P, J], F32, name="neg_c")
+            shifts[(g, j0)] = neg_c
+            nc.gpsimd.tensor_tensor(
+                out=neg_c[:, 0:n], in0=lnq[(g, j0)][:, 0:n], in1=w[:, 0:n], op=ALU.subtract
+            )
+
+        def ln_table(g, j0, j1):
+            y = small.tile([P, J], F32, name="y")
+            lne[(g, j0)] = y
+            nc.scalar.activation(out=y[:, 0 : j1 - j0], in_=esums[g][:, j0:j1], func=ACT.Ln)
+
+        def ln_table_shift(g, j0, j1):
+            n = j1 - j0
+            neg_c = small.tile([P, J], F32, name="neg_c")
+            shifts[(g, j0)] = neg_c
+            nc.vector.tensor_tensor(
+                out=neg_c[:, 0:n], in0=negs[g][:, j0:j1], in1=lne[(g, j0)][:, 0:n], op=ALU.subtract
+            )
+
+        def subtract_store(g, h, key, on_vector):
+            lt = lts[g]
+            for jj in range(JH):
+                j = h * JH + jj
+                shift = shifts[key][:, j - key[1] : j - key[1] + 1]
+                if on_vector:
                     nc.vector.tensor_scalar(
-                        out=zt[:, kt, :],
-                        in0=zt[:, kt, :],
-                        scalar1=a[:, kt : kt + 1],
-                        scalar2=bb[:, kt : kt + 1],
-                        op0=ALU.mult,
-                        op1=ALU.add,
+                        out=lt[:, j, :], in0=lt[:, j, :], scalar1=shift, scalar2=None, op0=ALU.add
                     )
                 else:
                     nc.scalar.activation(
-                        out=zt[:, kt, :],
-                        in_=zt[:, kt, :],
-                        func=ACT.Relu,
-                        bias=bb[:, kt : kt + 1],
-                        scale=a[:, kt : kt + 1],
+                        out=lt[:, j, :], in_=lt[:, j, :], func=ACT.Identity, bias=shift, scale=1.0
                     )
-
-            neg_m = small.tile([P, J], F32, name="neg_m")
-            esum = small.tile([P, J], F32, name="esum")
-            ls = []
-            for h in range(2):
-                gh = grp.tile([P, 2, UB, 4], BF16, tag="gr", name="gh", align_bytes=64)
-                for c in range(2):
-                    dst = gh[:, c, :, :].rearrange("p (n i) t -> p n t i", i=4)
-                    src = zt[:, 4 * c : 4 * c + 4, h * UB : (h + 1) * UB].rearrange(
-                        "p t (n i) -> p n t i", i=4
-                    )
-                    if (h, c) in R_V:
-                        nc.vector.tensor_scalar(
-                            out=dst, in0=src, scalar1=0.0, scalar2=None, op0=ALU.max
-                        )
-                    else:
-                        nc.scalar.activation(out=dst, in_=src, func=ACT.Relu)
-                cd = cod.tile([P, 2 * UB], U32, tag="cd", name="cd", align_bytes=64)
-                sc = cod.tile([P, 2 * UB], U8, tag="sc", name="sc", align_bytes=64)
-                nc.vector.quantize_mx(
-                    out=cd[:].bitcast(FP8X4),
-                    scales=sc[:],
-                    in_=gh[:].rearrange("p c b t -> p (c b t)"),
-                )
-
-                lt = stream.tile([P, JH, C], F32, tag="st", name="lt")
-                ls.append(lt)
-                for jj in range(JH):
-                    acc = psum.tile([P, C], F32, tag="ps", name="acc")
-                    for c in range(2):
-                        col = c * UB + jj * P
-                        nc.tensor.matmul_mx(
-                            out=acc[:],
-                            lhsT=cd[:, col : col + P].bitcast(FP8X4),
-                            lhsT_scale=sc[:, col : col + P],
-                            rhs=wcodes[:, c * C : (c + 1) * C].bitcast(FP8X4),
-                            rhs_scale=wscl[:, c * C : (c + 1) * C],
-                            start=(c == 0),
-                            stop=(c == 1),
-                        )
-                    nc.vector.tensor_tensor(out=lt[:, jj, :], in0=acc[:], in1=bias_bc[:], op=ALU.add)
-                nc.vector.tensor_reduce(
-                    out=neg_m[:, h * JH : (h + 1) * JH], in_=lt[:], axis=AX.X, op=ALU.max, negate=True
-                )
-                for jj in range(JH):
-                    j = h * JH + jj
-                    nc.scalar.activation(
-                        out=junk_e[:],
-                        in_=lt[:, jj, :],
-                        func=ACT.Exp,
-                        bias=neg_m[:, j : j + 1],
-                        scale=1.0,
-                        accum_out=esum[:, j : j + 1],
-                    )
-
-            r_pos = small.tile([P, J], F32, name="r_pos")
-            nc.gpsimd.tensor_tensor(out=r_pos[:], in0=esum[:], in1=pe_pos[:], op=ALU.pow)
-            r_neg = small.tile([P, J], F32, name="r_neg")
-            nc.gpsimd.tensor_tensor(out=r_neg[:], in0=esum[:], in1=pe_neg[:], op=ALU.pow)
-            t = small.tile([P, J], F32, name="t")
-            nc.gpsimd.tensor_tensor(out=t[:], in0=r_pos[:], in1=r_neg[:], op=ALU.subtract)
-            e = small.tile([P, J], F32, name="e")
-            nc.scalar.activation(out=e[:], in_=t[:], func=ACT.Exp, scale=-0.5 * ROOT)
-            q = small.tile([P, J], F32, name="q")
-            nc.gpsimd.tensor_scalar(
-                out=q[:], in0=t[:], scalar1=-0.5 * ROOT, scalar2=1.0, op0=ALU.mult, op1=ALU.add
+            u = 2 * g + h
+            nc.sync.dma_start(
+                out=out[u * UB : (u + 1) * UB, :].rearrange("(p j) c -> p j c", j=JH),
+                in_=lt[:, h * JH : (h + 1) * JH, :],
             )
-            q2 = small.tile([P, J], F32, name="q2")
-            nc.gpsimd.tensor_tensor(out=q2[:], in0=q[:], in1=neg_m[:], op=ALU.add)
-            w = small.tile([P, J], F32, name="w")
-            nc.gpsimd.tensor_tensor(out=w[:], in0=esum[:], in1=e[:], op=ALU.mult)
-            neg_c = small.tile([P, J], F32, name="neg_c")
-            nc.gpsimd.tensor_tensor(out=neg_c[:], in0=q2[:], in1=w[:], op=ALU.subtract)
 
-            for h in range(2):
-                lt = ls[h]
-                u = 2 * g + h
-                for jj in range(JH):
-                    j = h * JH + jj
-                    if j in E4_V:
-                        nc.vector.tensor_scalar(
-                            out=lt[:, jj, :],
-                            in0=lt[:, jj, :],
-                            scalar1=neg_c[:, j : j + 1],
-                            scalar2=None,
-                            op0=ALU.add,
-                        )
-                    else:
-                        nc.scalar.activation(
-                            out=lt[:, jj, :],
-                            in_=lt[:, jj, :],
-                            func=ACT.Identity,
-                            bias=neg_c[:, j : j + 1],
-                            scale=1.0,
-                        )
-                nc.sync.dma_start(
-                    out=out[u * UB : (u + 1) * UB, :].rearrange("(p j) c -> p j c", j=JH),
-                    in_=lt[:],
-                )
+        affine(0, range(KT))
+        regroup(0)
+        regroup(1)
+        quant(0)
+        mx(0)
+        affine(1, range(KT))
+        for v in range(U + 1):
+            if v + 1 < U:
+                quant(v + 1)
+                mx(v + 1)
+            if v < U:
+                bias_max(v)
+            if v >= 1:
+                expsum(v - 1)
+            gf, odd = divmod(v - 2, 2)
+            if v >= 2 and odd == 0 and gf < G - 1:
+                ln_guess(gf, 0, J)
+            if v >= 3 and odd == 1 and gf < G - 1:
+                ln_step(gf, 0, J)
+            if v == U - 1:
+                ln_guess(G - 1, 0, JH)
+            if v == U:
+                ln_step(G - 1, 0, JH)
+                ln_table(G - 1, JH, J)
+            if v + 2 < U:
+                regroup(v + 2)
+            if v + 4 < U:
+                half = range(0, 4) if v % 2 == 0 else range(4, KT)
+                affine((v + 4) // 2, half)
+            if v >= 3 and odd == 1 and gf < G - 1:
+                subtract_store(gf, 0, (gf, 0), False)
+            if v >= 4 and odd == 0 and gf - 1 < G - 1:
+                subtract_store(gf - 1, 1, (gf - 1, 0), v == U)
+            if v == U:
+                subtract_store(G - 1, 0, (G - 1, 0), True)
+                ln_table_shift(G - 1, JH, J)
+                subtract_store(G - 1, 1, (G - 1, JH), True)

@@ -30,6 +30,7 @@ BN_EPS = 1e-5
 ROOT = 1024.0
 N_WARM = 12
 R_V = ((0, 0), (1, 1), (3, 0))
+GRAM_RUN = 2
 U_QW = 4
 
 FLOPS = 2 * B * K * C
@@ -97,6 +98,7 @@ def tile_binarymlp_pb_t_kernel(tc, z2, g2, beta2, W3, b3, out):
 
         zts = []
         gw = None
+        gram_jobs = [(i, jj) for i in range(NG) for jj in range(JH)]
         for u in range(U):
             g, h = divmod(u, 2)
             if h == 0:
@@ -110,21 +112,20 @@ def tile_binarymlp_pb_t_kernel(tc, z2, g2, beta2, W3, b3, out):
             if u == 0:
                 wn = big.tile([P, C // P, K], BF16, tag="big", name="wn")
                 nc.sync.dma_start(out=wn[:], in_=W3.rearrange("(t p) k -> p t k", p=P))
-            for i in range(NG):
-                ks = slice((KS + i) * P, (KS + i + 1) * P)
-                for jj in range(JH):
-                    nc.tensor.matmul(
-                        out=grams[i][:],
-                        lhsT=zn[:, jj, ks],
-                        rhs=zn[:, jj, ks],
-                        start=(u == 0 and jj == 0),
-                        stop=(u == U - 1 and jj == JH - 1),
-                    )
             for kt in range(KT):
                 ks = slice(kt * P, (kt + 1) * P)
                 pt = psum.tile([P, UB], BF16, tag="ps", name="pt")
                 for jj in range(JH):
                     nc.tensor.transpose(pt[:, jj * P : (jj + 1) * P], zn[:, jj, ks], ident[:])
+                for i, jj in gram_jobs[GRAM_RUN * kt : GRAM_RUN * (kt + 1)]:
+                    gs = slice((KS + i) * P, (KS + i + 1) * P)
+                    nc.tensor.matmul(
+                        out=grams[i][:],
+                        lhsT=zn[:, jj, gs],
+                        rhs=zn[:, jj, gs],
+                        start=(u == 0 and jj == 0),
+                        stop=(u == U - 1 and jj == JH - 1),
+                    )
                 nc.vector.tensor_scalar(
                     out=zt[:, kt, h * UB : (h + 1) * UB],
                     in0=pt[:],
@@ -149,7 +150,7 @@ def tile_binarymlp_pb_t_kernel(tc, z2, g2, beta2, W3, b3, out):
                             func=ACT.Square,
                             accum_out=sq[:, kt, g : g + 1],
                         )
-                if u == U - 1 and kt == 1:
+                if u == U - 1 and kt == KT - 2:
                     for i in range(NG):
                         nc.vector.scalar_tensor_tensor(
                             out=junk_d[:],
@@ -283,7 +284,7 @@ def tile_binarymlp_pb_t_kernel(tc, z2, g2, beta2, W3, b3, out):
                         stop=(c == 1),
                     )
 
-        def bias_max(u):
+        def add_bias(u):
             g, h = divmod(u, 2)
             if h == 0:
                 lts[g] = big.tile([P, J, C], F32, tag="big", name="lt")
@@ -294,9 +295,12 @@ def tile_binarymlp_pb_t_kernel(tc, z2, g2, beta2, W3, b3, out):
                 nc.vector.tensor_tensor(
                     out=lt[:, h * JH + jj, :], in0=accs[(u, jj)][:], in1=bias_bc[:], op=ALU.add
                 )
+
+        def row_max(u):
+            g, h = divmod(u, 2)
             nc.vector.tensor_reduce(
                 out=negs[g][:, h * JH : (h + 1) * JH],
-                in_=lt[:, h * JH : (h + 1) * JH, :],
+                in_=lts[g][:, h * JH : (h + 1) * JH, :],
                 axis=AX.X,
                 op=ALU.max,
                 negate=True,
@@ -404,7 +408,7 @@ def tile_binarymlp_pb_t_kernel(tc, z2, g2, beta2, W3, b3, out):
                 quant(v + 1)
                 mx(v + 1)
             if v < U:
-                bias_max(v)
+                add_bias(v)
             if v >= 1:
                 expsum(v - 1)
             gf, odd = divmod(v - 2, 2)
@@ -422,6 +426,8 @@ def tile_binarymlp_pb_t_kernel(tc, z2, g2, beta2, W3, b3, out):
             if v + 4 < U:
                 half = range(0, 4) if v % 2 == 0 else range(4, KT)
                 affine((v + 4) // 2, half)
+            if v < U:
+                row_max(v)
             if v >= 3 and odd == 1 and gf < G - 1:
                 subtract_store(gf, 0, (gf, 0), False)
             if v >= 4 and odd == 0 and gf - 1 < G - 1:

@@ -29,7 +29,7 @@ KS = KT - NG
 BN_EPS = 1e-5
 ROOT = 1024.0
 N_WARM = 12
-R_V = ((0, 0), (1, 1), (3, 0))
+R_V = ()
 GRAM_RUN = 2
 U_QW = 4
 
@@ -378,14 +378,23 @@ def tile_binarymlp_pb_t_kernel(tc, z2, g2, beta2, W3, b3, out):
                 out=neg_c[:, 0:n], in0=negs[g][:, j0:j1], in1=lne[(g, j0)][:, 0:n], op=ALU.subtract
             )
 
-        def subtract_store(g, h, key, on_vector):
+        def subtract_store(g, h, key, engine):
             lt = lts[g]
             for jj in range(JH):
                 j = h * JH + jj
                 shift = shifts[key][:, j - key[1] : j - key[1] + 1]
-                if on_vector:
+                if engine == "V":
                     nc.vector.tensor_scalar(
                         out=lt[:, j, :], in0=lt[:, j, :], scalar1=shift, scalar2=None, op0=ALU.add
+                    )
+                elif engine == "G":
+                    nc.gpsimd.tensor_scalar(
+                        out=lt[:, j, :],
+                        in0=lt[:, j, :],
+                        scalar1=1.0,
+                        scalar2=shift,
+                        op0=ALU.mult,
+                        op1=ALU.add,
                     )
                 else:
                     nc.scalar.activation(
@@ -429,10 +438,10 @@ def tile_binarymlp_pb_t_kernel(tc, z2, g2, beta2, W3, b3, out):
             if v < U:
                 row_max(v)
             if v >= 3 and odd == 1 and gf < G - 1:
-                subtract_store(gf, 0, (gf, 0), False)
+                subtract_store(gf, 0, (gf, 0), "G")
             if v >= 4 and odd == 0 and gf - 1 < G - 1:
-                subtract_store(gf - 1, 1, (gf - 1, 0), v == U)
+                subtract_store(gf - 1, 1, (gf - 1, 0), "V" if v == U else "G")
             if v == U:
-                subtract_store(G - 1, 0, (G - 1, 0), True)
+                subtract_store(G - 1, 0, (G - 1, 0), "V")
                 ln_table_shift(G - 1, JH, J)
-                subtract_store(G - 1, 1, (G - 1, JH), True)
+                subtract_store(G - 1, 1, (G - 1, JH), "V")

@@ -29,9 +29,9 @@ KS = KT - NG
 BN_EPS = 1e-5
 ROOT = 1024.0
 N_WARM = 12
-R_V = ()
+U_W = 2
+W_EARLY = 2
 GRAM_RUN = 2
-U_QW = 4
 
 FLOPS = 2 * B * K * C
 
@@ -47,6 +47,13 @@ def tile_binarymlp_pb_t_kernel(tc, z2, g2, beta2, W3, b3, out):
         psum = ctx.enter_context(tc.psum_pool(name="psum", bufs=8))
         ctx.enter_context(tc.manual_schedule())
 
+        brow = const.tile([P, C], BF16, name="brow")
+        nc.vector.memset(brow[:], 0.0)
+        vecs = const.tile([P, P], BF16, name="vecs")
+        nc.vector.memset(vecs[:], 0.0)
+        nc.sync.dma_start(out=brow[0:1, :], in_=b3.rearrange("(o c) -> o c", o=1))
+        nc.sync.dma_start(out=vecs[0:KT, :], in_=g2.rearrange("(t p) -> t p", p=P))
+        nc.sync.dma_start(out=vecs[KT : 2 * KT, :], in_=beta2.rearrange("(t p) -> t p", p=P))
         wcodes = const.tile([P, 2 * C], U32, name="wcodes", align_bytes=64)
         wscl = const.tile([P, 2 * C], U8, name="wscl", align_bytes=64)
         nc.vector.memset(wcodes[:, 0:C].bitcast(I32), 0)
@@ -72,22 +79,15 @@ def tile_binarymlp_pb_t_kernel(tc, z2, g2, beta2, W3, b3, out):
         make_identity(nc, ident[:])
         ones = const.tile([P, P], BF16, name="ones")
         nc.vector.memset(ones[:], 1.0)
-        brow = const.tile([P, C], BF16, name="brow")
-        nc.vector.memset(brow[:], 0.0)
-        vecs = const.tile([P, P], BF16, name="vecs")
-        nc.vector.memset(vecs[:], 0.0)
-        nc.gpsimd.dma_start(out=brow[0:1, :], in_=b3.rearrange("(o c) -> o c", o=1))
-        nc.gpsimd.dma_start(out=vecs[0:KT, :], in_=g2.rearrange("(t p) -> t p", p=P))
-        nc.gpsimd.dma_start(out=vecs[KT : 2 * KT, :], in_=beta2.rearrange("(t p) -> t p", p=P))
         pe_pos = const.tile([P, J], F32, name="pe_pos")
         nc.gpsimd.memset(pe_pos[:], 1.0 / ROOT)
         pe_neg = const.tile([P, J], F32, name="pe_neg")
         nc.gpsimd.memset(pe_neg[:], -1.0 / ROOT)
 
         s1 = const.tile([P, KT, U], F32, name="s1")
-        sq = const.tile([P, KS, G + 1], F32, name="sq")
+        sq = const.tile([P, KS, U], F32, name="sq")
         ssq = const.tile([P, KT], F32, name="ssq")
-        junk_s = const.tile([P, GB], BF16, name="junk_s")
+        junk_s = const.tile([P, UB], BF16, name="junk_s")
         junk_e = const.tile([P, C], BF16, name="junk_e")
         junk_d = const.tile([P, P], F32, name="junk_d")
         gb = const.tile([P, 2 * KT], F32, name="gb")
@@ -96,21 +96,27 @@ def tile_binarymlp_pb_t_kernel(tc, z2, g2, beta2, W3, b3, out):
         for i in range(NG):
             grams.append(psum.tile([P, P], F32, tag="ps", name="gram%d" % i))
 
+        pv = psum.tile([P, P], BF16, tag="ps", name="pv")
+        nc.tensor.transpose(pv[:], vecs[:], ident[:])
+        nc.vector.tensor_copy(out=gb[:], in_=pv[:, 0 : 2 * KT])
+        pb = psum.tile([P, C], F32, tag="ps", name="pb")
+        nc.tensor.matmul(out=pb[:], lhsT=ones[:], rhs=brow[:], start=True, stop=True)
+        nc.scalar.copy(out=bias_bc[:], in_=pb[:])
+
         zts = []
-        gw = None
         gram_jobs = [(i, jj) for i in range(NG) for jj in range(JH)]
         for u in range(U):
             g, h = divmod(u, 2)
             if h == 0:
-                zts.append(big.tile([P, KT, GB], BF16, tag="big", name="zt%d" % g))
+                zts.append(big.tile([P, KT, GB], BF16, tag="big", name="zt%d" % g, align_bytes=64))
             zt = zts[g]
-            zn = big.tile([P, JH, K], BF16, tag="big", name="zn")
+            zn = big.tile([P, JH, K], BF16, tag="big", name="zn", align_bytes=64)
             nc.sync.dma_start(
                 out=zn[:],
                 in_=z2[u * UB : (u + 1) * UB, :].rearrange("(p j) k -> p j k", j=JH),
             )
-            if u == 0:
-                wn = big.tile([P, C // P, K], BF16, tag="big", name="wn")
+            if u == U_W:
+                wn = big.tile([P, C // P, K], BF16, tag="big", name="wn", align_bytes=64)
                 nc.sync.dma_start(out=wn[:], in_=W3.rearrange("(t p) k -> p t k", p=P))
             for kt in range(KT):
                 ks = slice(kt * P, (kt + 1) * P)
@@ -136,20 +142,12 @@ def tile_binarymlp_pb_t_kernel(tc, z2, g2, beta2, W3, b3, out):
                     accum_out=s1[:, kt, u : u + 1],
                 )
                 if kt < KS:
-                    if g == G - 1:
-                        nc.scalar.activation(
-                            out=junk_s[:, 0:UB],
-                            in_=zt[:, kt, h * UB : (h + 1) * UB],
-                            func=ACT.Square,
-                            accum_out=sq[:, kt, g + h : g + h + 1],
-                        )
-                    elif h == 1:
-                        nc.scalar.activation(
-                            out=junk_s[:],
-                            in_=zt[:, kt, :],
-                            func=ACT.Square,
-                            accum_out=sq[:, kt, g : g + 1],
-                        )
+                    nc.scalar.activation(
+                        out=junk_s[:],
+                        in_=zt[:, kt, h * UB : (h + 1) * UB],
+                        func=ACT.Square,
+                        accum_out=sq[:, kt, u : u + 1],
+                    )
                 if u == U - 1 and kt == KT - 2:
                     for i in range(NG):
                         nc.vector.scalar_tensor_tensor(
@@ -162,35 +160,21 @@ def tile_binarymlp_pb_t_kernel(tc, z2, g2, beta2, W3, b3, out):
                             accum_out=ssq[:, KS + i : KS + i + 1],
                         )
 
-            if u == 0:
-                pv = psum.tile([P, P], BF16, tag="ps", name="pv")
-                nc.tensor.transpose(pv[:], vecs[:], ident[:])
-                nc.vector.tensor_copy(out=gb[:], in_=pv[:, 0 : 2 * KT])
-                pb = psum.tile([P, C], F32, tag="ps", name="pb")
-                nc.tensor.matmul(out=pb[:], lhsT=ones[:], rhs=brow[:], start=True, stop=True)
-                nc.scalar.copy(out=bias_bc[:], in_=pb[:])
-                wt = big.tile([P, KT, C], BF16, tag="big", name="wt")
-                for kt in range(KT):
-                    ks = slice(kt * P, (kt + 1) * P)
-                    pw = psum.tile([P, C], BF16, tag="ps", name="pw")
-                    for t in range(C // P):
-                        nc.tensor.transpose(pw[:, t * P : (t + 1) * P], wn[:, t, ks], ident[:])
-                    nc.scalar.copy(out=wt[:, kt, :], in_=pw[:])
-                gw = grp.tile([P, 2, C, 4], BF16, tag="gr", name="gw", align_bytes=64)
-                nc.gpsimd.tensor_scalar(
-                    out=gw[:],
-                    in0=wt[:].rearrange("p (c t) n -> p c n t", t=4),
-                    scalar1=1.0,
-                    scalar2=0.0,
-                    op0=ALU.mult,
-                    op1=ALU.add,
-                )
-            if u == U_QW:
-                nc.vector.quantize_mx(
-                    out=wcodes[:].bitcast(FP8X4),
-                    scales=wscl[:],
-                    in_=gw[:].rearrange("p c n t -> p (c n t)"),
-                )
+
+        gw = big.tile([P, 2, C, 4], BF16, tag="big", name="gw", align_bytes=64)
+
+        def w_bank(n):
+            c, ct = divmod(n, C // P)
+            pw = psum.tile([P, 4, P], BF16, tag="ps", name="pw")
+            for t in range(4):
+                kt = 4 * c + t
+                nc.tensor.transpose(pw[:, t, :], wn[:, ct, kt * P : (kt + 1) * P], ident[:])
+            nc.scalar.copy(
+                out=gw[:, c, ct * P : (ct + 1) * P, :], in_=pw[:].rearrange("p t n -> p n t")
+            )
+
+        for n in range(W_EARLY):
+            w_bank(n)
 
         ssum = const.tile([P, KT], F32, name="ssum")
         nc.vector.tensor_reduce(out=ssum[:], in_=s1[:], axis=AX.X, op=ALU.add)
@@ -209,6 +193,8 @@ def tile_binarymlp_pb_t_kernel(tc, z2, g2, beta2, W3, b3, out):
         )
         sd = const.tile([P, KT], F32, name="sd")
         nc.scalar.activation(out=sd[:], in_=ve[:], func=ACT.Sqrt)
+        for n in range(W_EARLY, 2 * C // P):
+            w_bank(n)
         mean = const.tile([P, KT], F32, name="mean")
         nc.vector.tensor_scalar(out=mean[:], in0=ssum[:], scalar1=1.0 / B, scalar2=None, op0=ALU.mult)
         rstd = const.tile([P, KT], F32, name="rstd")
@@ -252,7 +238,7 @@ def tile_binarymlp_pb_t_kernel(tc, z2, g2, beta2, W3, b3, out):
                 src = zts[g][:, 4 * c : 4 * c + 4, h * UB : (h + 1) * UB].rearrange(
                     "p t (n i) -> p n t i", i=4
                 )
-                if (u % 4, c) in R_V:
+                if u == 0:
                     nc.vector.tensor_scalar(out=dst, in0=src, scalar1=0.0, scalar2=None, op0=ALU.max)
                 else:
                     nc.scalar.activation(out=dst, in_=src, func=ACT.Relu)
@@ -284,23 +270,23 @@ def tile_binarymlp_pb_t_kernel(tc, z2, g2, beta2, W3, b3, out):
                         stop=(c == 1),
                     )
 
-        def add_bias(u):
+        def add_bias(u, tiles):
             g, h = divmod(u, 2)
-            if h == 0:
-                lts[g] = big.tile([P, J, C], F32, tag="big", name="lt")
+            if h == 0 and tiles[0] == 0:
+                lts[g] = big.tile([P, J, C], F32, tag="big", name="lt", align_bytes=64)
                 negs[g] = small.tile([P, J], F32, name="neg_m")
                 esums[g] = small.tile([P, J], F32, name="esum")
             lt = lts[g]
-            for jj in range(JH):
+            for jj in tiles:
                 nc.vector.tensor_tensor(
                     out=lt[:, h * JH + jj, :], in0=accs[(u, jj)][:], in1=bias_bc[:], op=ALU.add
                 )
 
-        def row_max(u):
+        def row_max(u, jj0, jj1):
             g, h = divmod(u, 2)
             nc.vector.tensor_reduce(
-                out=negs[g][:, h * JH : (h + 1) * JH],
-                in_=lts[g][:, h * JH : (h + 1) * JH, :],
+                out=negs[g][:, h * JH + jj0 : h * JH + jj1],
+                in_=lts[g][:, h * JH + jj0 : h * JH + jj1, :],
                 axis=AX.X,
                 op=ALU.max,
                 negate=True,
@@ -378,11 +364,12 @@ def tile_binarymlp_pb_t_kernel(tc, z2, g2, beta2, W3, b3, out):
                 out=neg_c[:, 0:n], in0=negs[g][:, j0:j1], in1=lne[(g, j0)][:, 0:n], op=ALU.subtract
             )
 
-        def subtract_store(g, h, key, engine):
+        def subtract_store(g, h, key, engines):
             lt = lts[g]
             for jj in range(JH):
                 j = h * JH + jj
                 shift = shifts[key][:, j - key[1] : j - key[1] + 1]
+                engine = engines[jj]
                 if engine == "V":
                     nc.vector.tensor_scalar(
                         out=lt[:, j, :], in0=lt[:, j, :], scalar1=shift, scalar2=None, op0=ALU.add
@@ -409,6 +396,11 @@ def tile_binarymlp_pb_t_kernel(tc, z2, g2, beta2, W3, b3, out):
         affine(0, range(KT))
         regroup(0)
         regroup(1)
+        nc.vector.quantize_mx(
+            out=wcodes[:].bitcast(FP8X4),
+            scales=wscl[:],
+            in_=gw[:].rearrange("p c n t -> p (c n t)"),
+        )
         quant(0)
         mx(0)
         affine(1, range(KT))
@@ -416,32 +408,35 @@ def tile_binarymlp_pb_t_kernel(tc, z2, g2, beta2, W3, b3, out):
             if v + 1 < U:
                 quant(v + 1)
                 mx(v + 1)
-            if v < U:
-                add_bias(v)
+            if v < U - 1:
+                add_bias(v, range(JH))
+            if v == U - 1:
+                for jj in range(JH):
+                    add_bias(v, range(jj, jj + 1))
+                    if jj >= 1:
+                        row_max(v, jj - 1, jj)
+                row_max(v, JH - 1, JH)
             if v >= 1:
                 expsum(v - 1)
             gf, odd = divmod(v - 2, 2)
             if v >= 2 and odd == 0 and gf < G - 1:
                 ln_guess(gf, 0, J)
-            if v >= 3 and odd == 1 and gf < G - 1:
+            if v >= 3 and odd == 1:
                 ln_step(gf, 0, J)
-            if v == U - 1:
-                ln_guess(G - 1, 0, JH)
             if v == U:
-                ln_step(G - 1, 0, JH)
-                ln_table(G - 1, JH, J)
+                ln_table(G - 1, 0, J)
             if v + 2 < U:
                 regroup(v + 2)
             if v + 4 < U:
                 half = range(0, 4) if v % 2 == 0 else range(4, KT)
                 affine((v + 4) // 2, half)
-            if v < U:
-                row_max(v)
-            if v >= 3 and odd == 1 and gf < G - 1:
-                subtract_store(gf, 0, (gf, 0), "G")
-            if v >= 4 and odd == 0 and gf - 1 < G - 1:
-                subtract_store(gf - 1, 1, (gf - 1, 0), "V" if v == U else "G")
+            if v < U - 1:
+                row_max(v, 0, JH)
+            if v >= 3 and odd == 1:
+                subtract_store(gf, 0, (gf, 0), "GGGG" if v < U - 2 else "SSSS")
+            if v >= 4 and odd == 0:
+                subtract_store(gf - 1, 1, (gf - 1, 0), "GGGG" if v < U - 2 else "VVVV")
             if v == U:
-                subtract_store(G - 1, 0, (G - 1, 0), "V")
-                ln_table_shift(G - 1, JH, J)
-                subtract_store(G - 1, 1, (G - 1, JH), "V")
+                ln_table_shift(G - 1, 0, J)
+                subtract_store(G - 1, 0, (G - 1, 0), "VVVV")
+                subtract_store(G - 1, 1, (G - 1, 0), "SSVV")

@@ -29,9 +29,10 @@ KS = KT - NG
 BN_EPS = 1e-5
 ROOT = 1024.0
 N_WARM = 12
-U_W = 2
+R_V_COLS = 128
+G_W = 1
 W_EARLY = 2
-GRAM_RUN = 2
+GRAM_RUN = 4
 
 FLOPS = 2 * B * K * C
 
@@ -84,10 +85,13 @@ def tile_binarymlp_pb_t_kernel(tc, z2, g2, beta2, W3, b3, out):
         pe_neg = const.tile([P, J], F32, name="pe_neg")
         nc.gpsimd.memset(pe_neg[:], -1.0 / ROOT)
 
-        s1 = const.tile([P, KT, U], F32, name="s1")
-        sq = const.tile([P, KS, U], F32, name="sq")
+        s1 = const.tile([P, KT, G], F32, name="s1")
+        sq = const.tile([P, KS, G], F32, name="sq")
+        nc.vector.memset(sq[:], 0.0)
+        sqv = const.tile([P, G // 2], F32, name="sqv")
+        junk_v = const.tile([P, GB], BF16, name="junk_v")
         ssq = const.tile([P, KT], F32, name="ssq")
-        junk_s = const.tile([P, UB], BF16, name="junk_s")
+        junk_s = const.tile([P, GB], BF16, name="junk_s")
         junk_e = const.tile([P, C], BF16, name="junk_e")
         junk_d = const.tile([P, P], F32, name="junk_d")
         gb = const.tile([P, 2 * KT], F32, name="gb")
@@ -104,51 +108,64 @@ def tile_binarymlp_pb_t_kernel(tc, z2, g2, beta2, W3, b3, out):
         nc.scalar.copy(out=bias_bc[:], in_=pb[:])
 
         zts = []
-        gram_jobs = [(i, jj) for i in range(NG) for jj in range(JH)]
-        for u in range(U):
-            g, h = divmod(u, 2)
-            if h == 0:
-                zts.append(big.tile([P, KT, GB], BF16, tag="big", name="zt%d" % g, align_bytes=64))
-            zt = zts[g]
-            zn = big.tile([P, JH, K], BF16, tag="big", name="zn", align_bytes=64)
-            nc.sync.dma_start(
-                out=zn[:],
-                in_=z2[u * UB : (u + 1) * UB, :].rearrange("(p j) k -> p j k", j=JH),
-            )
-            if u == U_W:
+        gram_jobs = [(i, j) for i in range(NG) for j in range(J)]
+        for g in range(G):
+            zt = big.tile([P, KT, GB], BF16, tag="big", name="zt%d" % g, align_bytes=64)
+            zts.append(zt)
+            zn = big.tile([P, J, K], BF16, tag="big", name="zn", align_bytes=64)
+            pieces = 2 if g == 0 else 1
+            for piece in range(pieces):
+                cols = slice(piece * K // pieces, (piece + 1) * K // pieces)
+                for h in range(2):
+                    u = 2 * g + h
+                    nc.sync.dma_start(
+                        out=zn[:, h * JH : (h + 1) * JH, cols],
+                        in_=z2[u * UB : (u + 1) * UB, cols].rearrange("(p j) k -> p j k", j=JH),
+                    )
+            if g == G_W:
                 wn = big.tile([P, C // P, K], BF16, tag="big", name="wn", align_bytes=64)
                 nc.sync.dma_start(out=wn[:], in_=W3.rearrange("(t p) k -> p t k", p=P))
             for kt in range(KT):
                 ks = slice(kt * P, (kt + 1) * P)
-                pt = psum.tile([P, UB], BF16, tag="ps", name="pt")
-                for jj in range(JH):
-                    nc.tensor.transpose(pt[:, jj * P : (jj + 1) * P], zn[:, jj, ks], ident[:])
-                for i, jj in gram_jobs[GRAM_RUN * kt : GRAM_RUN * (kt + 1)]:
+                pt = psum.tile([P, GB], BF16, tag="ps", name="pt")
+                for j in range(J):
+                    nc.tensor.transpose(pt[:, j * P : (j + 1) * P], zn[:, j, ks], ident[:])
+                for i, j in gram_jobs[GRAM_RUN * kt : GRAM_RUN * (kt + 1)]:
                     gs = slice((KS + i) * P, (KS + i + 1) * P)
                     nc.tensor.matmul(
                         out=grams[i][:],
-                        lhsT=zn[:, jj, gs],
-                        rhs=zn[:, jj, gs],
-                        start=(u == 0 and jj == 0),
-                        stop=(u == U - 1 and jj == JH - 1),
+                        lhsT=zn[:, j, gs],
+                        rhs=zn[:, j, gs],
+                        start=(g == 0 and j == 0),
+                        stop=(g == G - 1 and j == J - 1),
                     )
                 nc.vector.tensor_scalar(
-                    out=zt[:, kt, h * UB : (h + 1) * UB],
+                    out=zt[:, kt, :],
                     in0=pt[:],
                     scalar1=1.0,
                     scalar2=None,
                     op0=ALU.mult,
                     op1=ALU.add,
-                    accum_out=s1[:, kt, u : u + 1],
+                    accum_out=s1[:, kt, g : g + 1],
                 )
-                if kt < KS:
+                if kt < KS - 1 or (kt == KS - 1 and g % 2 == 0):
                     nc.scalar.activation(
                         out=junk_s[:],
-                        in_=zt[:, kt, h * UB : (h + 1) * UB],
+                        in_=zt[:, kt, :],
                         func=ACT.Square,
-                        accum_out=sq[:, kt, u : u + 1],
+                        accum_out=sq[:, kt, g : g + 1],
                     )
-                if u == U - 1 and kt == KT - 2:
+                if kt == KS and g % 2 == 1:
+                    nc.vector.scalar_tensor_tensor(
+                        out=junk_v[:],
+                        in0=zt[:, KS - 1, :],
+                        scalar=1.0,
+                        in1=zt[:, KS - 1, :],
+                        op0=ALU.mult,
+                        op1=ALU.mult,
+                        accum_out=sqv[:, g // 2 : g // 2 + 1],
+                    )
+                if g == G - 1 and kt == KT - 2:
                     for i in range(NG):
                         nc.vector.scalar_tensor_tensor(
                             out=junk_d[:],
@@ -159,7 +176,6 @@ def tile_binarymlp_pb_t_kernel(tc, z2, g2, beta2, W3, b3, out):
                             op1=ALU.mult,
                             accum_out=ssq[:, KS + i : KS + i + 1],
                         )
-
 
         gw = big.tile([P, 2, C, 4], BF16, tag="big", name="gw", align_bytes=64)
 
@@ -178,7 +194,12 @@ def tile_binarymlp_pb_t_kernel(tc, z2, g2, beta2, W3, b3, out):
 
         ssum = const.tile([P, KT], F32, name="ssum")
         nc.vector.tensor_reduce(out=ssum[:], in_=s1[:], axis=AX.X, op=ALU.add)
+        sv = const.tile([P, 1], F32, name="sv")
+        nc.vector.tensor_reduce(out=sv[:], in_=sqv[:], axis=AX.X, op=ALU.add)
         nc.vector.tensor_reduce(out=ssq[:, 0:KS], in_=sq[:], axis=AX.X, op=ALU.add)
+        nc.vector.tensor_tensor(
+            out=ssq[:, KS - 1 : KS], in0=ssq[:, KS - 1 : KS], in1=sv[:], op=ALU.add
+        )
         m2 = const.tile([P, KT], F32, name="m2")
         nc.vector.scalar_tensor_tensor(
             out=m2[:], in0=ssum[:], scalar=1.0 / (B * B), in1=ssum[:], op0=ALU.mult, op1=ALU.mult
@@ -233,12 +254,16 @@ def tile_binarymlp_pb_t_kernel(tc, z2, g2, beta2, W3, b3, out):
             g, h = divmod(u, 2)
             gh = grp.tile([P, 2, UB, 4], BF16, tag="gr", name="gh", align_bytes=64)
             ghs[u] = gh
-            for c in range(2):
-                dst = gh[:, c, :, :].rearrange("p (n i) t -> p n t i", i=4)
-                src = zts[g][:, 4 * c : 4 * c + 4, h * UB : (h + 1) * UB].rearrange(
+            if u == 0:
+                shares = ((0, 0, UB, True), (1, 0, UB, True))
+            else:
+                shares = ((0, 0, UB, False), (1, 0, UB - R_V_COLS, False), (1, UB - R_V_COLS, UB, True))
+            for c, b0, b1, on_vector in shares:
+                dst = gh[:, c, b0:b1, :].rearrange("p (n i) t -> p n t i", i=4)
+                src = zts[g][:, 4 * c : 4 * c + 4, h * UB + b0 : h * UB + b1].rearrange(
                     "p t (n i) -> p n t i", i=4
                 )
-                if u == 0:
+                if on_vector:
                     nc.vector.tensor_scalar(out=dst, in0=src, scalar1=0.0, scalar2=None, op0=ALU.max)
                 else:
                     nc.scalar.activation(out=dst, in_=src, func=ACT.Relu)

@@ -28,8 +28,9 @@ NG = 3
 KS = KT - NG
 BN_EPS = 1e-5
 ROOT = 1024.0
-N_WARM = 12
-R_V_COLS = 128
+N_WARM = 16
+R_TAIL = 128
+BIG = 3.0e38
 G_W = 1
 W_EARLY = 2
 GRAM_RUN = 4
@@ -52,9 +53,6 @@ def tile_binarymlp_pb_t_kernel(tc, z2, g2, beta2, W3, b3, out):
         nc.vector.memset(brow[:], 0.0)
         vecs = const.tile([P, P], BF16, name="vecs")
         nc.vector.memset(vecs[:], 0.0)
-        nc.sync.dma_start(out=brow[0:1, :], in_=b3.rearrange("(o c) -> o c", o=1))
-        nc.sync.dma_start(out=vecs[0:KT, :], in_=g2.rearrange("(t p) -> t p", p=P))
-        nc.sync.dma_start(out=vecs[KT : 2 * KT, :], in_=beta2.rearrange("(t p) -> t p", p=P))
         wcodes = const.tile([P, 2 * C], U32, name="wcodes", align_bytes=64)
         wscl = const.tile([P, 2 * C], U8, name="wscl", align_bytes=64)
         nc.vector.memset(wcodes[:, 0:C].bitcast(I32), 0)
@@ -100,28 +98,22 @@ def tile_binarymlp_pb_t_kernel(tc, z2, g2, beta2, W3, b3, out):
         for i in range(NG):
             grams.append(psum.tile([P, P], F32, tag="ps", name="gram%d" % i))
 
-        pv = psum.tile([P, P], BF16, tag="ps", name="pv")
-        nc.tensor.transpose(pv[:], vecs[:], ident[:])
-        nc.vector.tensor_copy(out=gb[:], in_=pv[:, 0 : 2 * KT])
-        pb = psum.tile([P, C], F32, tag="ps", name="pb")
-        nc.tensor.matmul(out=pb[:], lhsT=ones[:], rhs=brow[:], start=True, stop=True)
-        nc.scalar.copy(out=bias_bc[:], in_=pb[:])
-
         zts = []
         gram_jobs = [(i, j) for i in range(NG) for j in range(J)]
         for g in range(G):
             zt = big.tile([P, KT, GB], BF16, tag="big", name="zt%d" % g, align_bytes=64)
             zts.append(zt)
             zn = big.tile([P, J, K], BF16, tag="big", name="zn", align_bytes=64)
-            pieces = 2 if g == 0 else 1
-            for piece in range(pieces):
-                cols = slice(piece * K // pieces, (piece + 1) * K // pieces)
-                for h in range(2):
-                    u = 2 * g + h
-                    nc.sync.dma_start(
-                        out=zn[:, h * JH : (h + 1) * JH, cols],
-                        in_=z2[u * UB : (u + 1) * UB, cols].rearrange("(p j) k -> p j k", j=JH),
-                    )
+            for h in range(2):
+                u = 2 * g + h
+                nc.sync.dma_start(
+                    out=zn[:, h * JH : (h + 1) * JH, :],
+                    in_=z2[u * UB : (u + 1) * UB, :].rearrange("(p j) k -> p j k", j=JH),
+                )
+            if g == 0:
+                nc.sync.dma_start(out=brow[0:1, :], in_=b3.rearrange("(o c) -> o c", o=1))
+                nc.sync.dma_start(out=vecs[0:KT, :], in_=g2.rearrange("(t p) -> t p", p=P))
+                nc.sync.dma_start(out=vecs[KT : 2 * KT, :], in_=beta2.rearrange("(t p) -> t p", p=P))
             if g == G_W:
                 wn = big.tile([P, C // P, K], BF16, tag="big", name="wn", align_bytes=64)
                 nc.sync.dma_start(out=wn[:], in_=W3.rearrange("(t p) k -> p t k", p=P))
@@ -176,6 +168,13 @@ def tile_binarymlp_pb_t_kernel(tc, z2, g2, beta2, W3, b3, out):
                             op1=ALU.mult,
                             accum_out=ssq[:, KS + i : KS + i + 1],
                         )
+            if g == 0:
+                pv = psum.tile([P, P], BF16, tag="ps", name="pv")
+                nc.tensor.transpose(pv[:], vecs[:], ident[:])
+                nc.vector.tensor_copy(out=gb[:], in_=pv[:, 0 : 2 * KT])
+                pb = psum.tile([P, C], F32, tag="ps", name="pb")
+                nc.tensor.matmul(out=pb[:], lhsT=ones[:], rhs=brow[:], start=True, stop=True)
+                nc.scalar.copy(out=bias_bc[:], in_=pb[:])
 
         gw = big.tile([P, 2, C, 4], BF16, tag="big", name="gw", align_bytes=64)
 
@@ -255,16 +254,25 @@ def tile_binarymlp_pb_t_kernel(tc, z2, g2, beta2, W3, b3, out):
             gh = grp.tile([P, 2, UB, 4], BF16, tag="gr", name="gh", align_bytes=64)
             ghs[u] = gh
             if u == 0:
-                shares = ((0, 0, UB, True), (1, 0, UB, True))
+                shares = ((0, 0, UB, "V"), (1, 0, UB, "S"))
             else:
-                shares = ((0, 0, UB, False), (1, 0, UB - R_V_COLS, False), (1, UB - R_V_COLS, UB, True))
-            for c, b0, b1, on_vector in shares:
+                shares = (
+                    (0, UB - R_TAIL, UB, "G"),
+                    (0, 0, UB - R_TAIL, "S"),
+                    (1, 0, UB - R_TAIL, "S"),
+                    (1, UB - R_TAIL, UB, "V"),
+                )
+            for c, b0, b1, engine in shares:
                 dst = gh[:, c, b0:b1, :].rearrange("p (n i) t -> p n t i", i=4)
                 src = zts[g][:, 4 * c : 4 * c + 4, h * UB + b0 : h * UB + b1].rearrange(
                     "p t (n i) -> p n t i", i=4
                 )
-                if on_vector:
+                if engine == "V":
                     nc.vector.tensor_scalar(out=dst, in0=src, scalar1=0.0, scalar2=None, op0=ALU.max)
+                elif engine == "G":
+                    nc.gpsimd.tensor_scalar(
+                        out=dst, in0=src, scalar1=BIG, scalar2=0.0, op0=ALU.min, op1=ALU.max
+                    )
                 else:
                     nc.scalar.activation(out=dst, in_=src, func=ACT.Relu)
 
@@ -389,7 +397,7 @@ def tile_binarymlp_pb_t_kernel(tc, z2, g2, beta2, W3, b3, out):
                 out=neg_c[:, 0:n], in0=negs[g][:, j0:j1], in1=lne[(g, j0)][:, 0:n], op=ALU.subtract
             )
 
-        def subtract_store(g, h, key, engines):
+        def subtract_store(g, h, key, engines, per_store):
             lt = lts[g]
             for jj in range(JH):
                 j = h * JH + jj
@@ -412,11 +420,12 @@ def tile_binarymlp_pb_t_kernel(tc, z2, g2, beta2, W3, b3, out):
                     nc.scalar.activation(
                         out=lt[:, j, :], in_=lt[:, j, :], func=ACT.Identity, bias=shift, scale=1.0
                     )
-            u = 2 * g + h
-            nc.sync.dma_start(
-                out=out[u * UB : (u + 1) * UB, :].rearrange("(p j) c -> p j c", j=JH),
-                in_=lt[:, h * JH : (h + 1) * JH, :],
-            )
+                if jj % per_store == per_store - 1:
+                    rows = out[(2 * g + h) * UB : (2 * g + h + 1) * UB, :]
+                    nc.sync.dma_start(
+                        out=rows.rearrange("(p j) c -> p j c", j=JH)[:, jj + 1 - per_store : jj + 1, :],
+                        in_=lt[:, j + 1 - per_store : j + 1, :],
+                    )
 
         affine(0, range(KT))
         regroup(0)
@@ -433,6 +442,8 @@ def tile_binarymlp_pb_t_kernel(tc, z2, g2, beta2, W3, b3, out):
             if v + 1 < U:
                 quant(v + 1)
                 mx(v + 1)
+            if v + 2 < U:
+                regroup(v + 2)
             if v < U - 1:
                 add_bias(v, range(JH))
             if v == U - 1:
@@ -450,18 +461,16 @@ def tile_binarymlp_pb_t_kernel(tc, z2, g2, beta2, W3, b3, out):
                 ln_step(gf, 0, J)
             if v == U:
                 ln_table(G - 1, 0, J)
-            if v + 2 < U:
-                regroup(v + 2)
             if v + 4 < U:
                 half = range(0, 4) if v % 2 == 0 else range(4, KT)
                 affine((v + 4) // 2, half)
             if v < U - 1:
                 row_max(v, 0, JH)
             if v >= 3 and odd == 1:
-                subtract_store(gf, 0, (gf, 0), "GGGG" if v < U - 2 else "SSSS")
+                subtract_store(gf, 0, (gf, 0), "GGGG" if v < U - 2 else "SSSS", JH)
             if v >= 4 and odd == 0:
-                subtract_store(gf - 1, 1, (gf - 1, 0), "GGGG" if v < U - 2 else "VVVV")
+                subtract_store(gf - 1, 1, (gf - 1, 0), "GGGG" if v < U - 2 else "VVVV", JH)
             if v == U:
                 ln_table_shift(G - 1, 0, J)
-                subtract_store(G - 1, 0, (G - 1, 0), "VVVV")
-                subtract_store(G - 1, 1, (G - 1, 0), "SSVV")
+                subtract_store(G - 1, 0, (G - 1, 0), "VVVV", JH)
+                subtract_store(G - 1, 1, (G - 1, 0), "SSVV", JH // 2)

@@ -30,7 +30,6 @@ BN_EPS = 1e-5
 ROOT = 1024.0
 N_WARM = 16
 R_TAIL = 128
-BIG = 3.0e38
 G_W = 1
 W_EARLY = 2
 GRAM_RUN = 4
@@ -256,12 +255,7 @@ def tile_binarymlp_pb_t_kernel(tc, z2, g2, beta2, W3, b3, out):
             if u == 0:
                 shares = ((0, 0, UB, "V"), (1, 0, UB, "S"))
             else:
-                shares = (
-                    (0, UB - R_TAIL, UB, "G"),
-                    (0, 0, UB - R_TAIL, "S"),
-                    (1, 0, UB - R_TAIL, "S"),
-                    (1, UB - R_TAIL, UB, "V"),
-                )
+                shares = ((0, 0, UB, "S"), (1, 0, UB - R_TAIL, "S"), (1, UB - R_TAIL, UB, "V"))
             for c, b0, b1, engine in shares:
                 dst = gh[:, c, b0:b1, :].rearrange("p (n i) t -> p n t i", i=4)
                 src = zts[g][:, 4 * c : 4 * c + 4, h * UB + b0 : h * UB + b1].rearrange(
@@ -269,10 +263,6 @@ def tile_binarymlp_pb_t_kernel(tc, z2, g2, beta2, W3, b3, out):
                 )
                 if engine == "V":
                     nc.vector.tensor_scalar(out=dst, in0=src, scalar1=0.0, scalar2=None, op0=ALU.max)
-                elif engine == "G":
-                    nc.gpsimd.tensor_scalar(
-                        out=dst, in0=src, scalar1=BIG, scalar2=0.0, op0=ALU.min, op1=ALU.max
-                    )
                 else:
                     nc.scalar.activation(out=dst, in_=src, func=ACT.Relu)
 

from contextlib import ExitStack

import concourse.mybir as mybir
from concourse.masks import make_identity

F32 = mybir.dt.float32
BF16 = mybir.dt.bfloat16
U32 = mybir.dt.uint32
U8 = mybir.dt.uint8
I32 = mybir.dt.int32
FP8X4 = mybir.dt.float8_e4m3fn_x4
ALU = mybir.AluOpType
ACT = mybir.ActivationFunctionType
AX = mybir.AxisListType

P = 128
B = 8192
K = 1024
C = 512
KT = K // P
G = 8
GB = B // G
U = 16
UB = B // U
JH = UB // P
J = GB // P
NG = 3
KS = KT - NG
BN_EPS = 1e-5
ROOT = 1024.0
N_WARM = 16
R_TAIL = 128
G_W = 1
W_EARLY = 2
GRAM_RUN = 4

FLOPS = 2 * B * K * C


def tile_binarymlp_pb_t_kernel(tc, z2, g2, beta2, W3, b3, out):
    nc = tc.nc
    with ExitStack() as ctx:
        const = ctx.enter_context(tc.tile_pool(name="const", bufs=1))
        big = ctx.enter_context(tc.tile_pool(name="big", bufs=11))
        grp = ctx.enter_context(tc.tile_pool(name="grp", bufs=2))
        cod = ctx.enter_context(tc.tile_pool(name="cod", bufs=4))
        small = ctx.enter_context(tc.tile_pool(name="small", bufs=4))
        psum = ctx.enter_context(tc.psum_pool(name="psum", bufs=8))
        ctx.enter_context(tc.manual_schedule())

        brow = const.tile([P, C], BF16, name="brow")
        nc.vector.memset(brow[:], 0.0)
        vecs = const.tile([P, P], BF16, name="vecs")
        nc.vector.memset(vecs[:], 0.0)
        wcodes = const.tile([P, 2 * C], U32, name="wcodes", align_bytes=64)
        wscl = const.tile([P, 2 * C], U8, name="wscl", align_bytes=64)
        nc.vector.memset(wcodes[:, 0:C].bitcast(I32), 0)
        nc.vector.memset(wscl[:, 0:C].bitcast(I32), 0)
        one = const.tile([P, 1], F32, name="one")
        nc.vector.memset(one[:], 1.0)
        warm = const.tile([P, 1], F32, name="warm")
        nc.scalar.activation(out=warm[:], in_=one[:], func=ACT.Sqrt)

        pwarm = psum.tile([P, C], F32, tag="ps", name="pwarm")
        for i in range(N_WARM):
            nc.tensor.matmul_mx(
                out=pwarm[:],
                lhsT=wcodes[:, 0:P].bitcast(FP8X4),
                lhsT_scale=wscl[:, 0:P],
                rhs=wcodes[:, 0:C].bitcast(FP8X4),
                rhs_scale=wscl[:, 0:C],
                start=True,
                stop=True,
            )

        ident = const.tile([P, P], BF16, name="ident")
        make_identity(nc, ident[:])
        ones = const.tile([P, P], BF16, name="ones")
        nc.vector.memset(ones[:], 1.0)
        pe_pos = const.tile([P, J], F32, name="pe_pos")
        nc.gpsimd.memset(pe_pos[:], 1.0 / ROOT)
        pe_neg = const.tile([P, J], F32, name="pe_neg")
        nc.gpsimd.memset(pe_neg[:], -1.0 / ROOT)

        s1 = const.tile([P, KT, G], F32, name="s1")
        sq = const.tile([P, KS, G], F32, name="sq")
        nc.vector.memset(sq[:], 0.0)
        sqv = const.tile([P, G // 2], F32, name="sqv")
        junk_v = const.tile([P, GB], BF16, name="junk_v")
        ssq = const.tile([P, KT], F32, name="ssq")
        junk_s = const.tile([P, GB], BF16, name="junk_s")
        junk_e = const.tile([P, C], BF16, name="junk_e")
        junk_d = const.tile([P, P], F32, name="junk_d")
        gb = const.tile([P, 2 * KT], F32, name="gb")
        bias_bc = const.tile([P, C], F32, name="bias_bc")
        grams = []
        for i in range(NG):
            grams.append(psum.tile([P, P], F32, tag="ps", name="gram%d" % i))

        zts = []
        gram_jobs = [(i, j) for i in range(NG) for j in range(J)]
        for g in range(G):
            zt = big.tile([P, KT, GB], BF16, tag="big", name="zt%d" % g, align_bytes=64)
            zts.append(zt)
            zn = big.tile([P, J, K], BF16, tag="big", name="zn", align_bytes=64)
            for h in range(2):
                u = 2 * g + h
                nc.sync.dma_start(
                    out=zn[:, h * JH : (h + 1) * JH, :],
                    in_=z2[u * UB : (u + 1) * UB, :].rearrange("(p j) k -> p j k", j=JH),
                )
            if g == 0:
                nc.sync.dma_start(out=brow[0:1, :], in_=b3.rearrange("(o c) -> o c", o=1))
                nc.sync.dma_start(out=vecs[0:KT, :], in_=g2.rearrange("(t p) -> t p", p=P))
                nc.sync.dma_start(out=vecs[KT : 2 * KT, :], in_=beta2.rearrange("(t p) -> t p", p=P))
            if g == G_W:
                wn = big.tile([P, C // P, K], BF16, tag="big", name="wn", align_bytes=64)
                nc.sync.dma_start(out=wn[:], in_=W3.rearrange("(t p) k -> p t k", p=P))
            for kt in range(KT):
                ks = slice(kt * P, (kt + 1) * P)
                pt = psum.tile([P, GB], BF16, tag="ps", name="pt")
                for j in range(J):
                    nc.tensor.transpose(pt[:, j * P : (j + 1) * P], zn[:, j, ks], ident[:])
                for i, j in gram_jobs[GRAM_RUN * kt : GRAM_RUN * (kt + 1)]:
                    gs = slice((KS + i) * P, (KS + i + 1) * P)
                    nc.tensor.matmul(
                        out=grams[i][:],
                        lhsT=zn[:, j, gs],
                        rhs=zn[:, j, gs],
                        start=(g == 0 and j == 0),
                        stop=(g == G - 1 and j == J - 1),
                    )
                nc.vector.tensor_scalar(
                    out=zt[:, kt, :],
                    in0=pt[:],
                    scalar1=1.0,
                    scalar2=None,
                    op0=ALU.mult,
                    op1=ALU.add,
                    accum_out=s1[:, kt, g : g + 1],
                )
                if kt < KS - 1 or (kt == KS - 1 and g % 2 == 0):
                    nc.scalar.activation(
                        out=junk_s[:],
                        in_=zt[:, kt, :],
                        func=ACT.Square,
                        accum_out=sq[:, kt, g : g + 1],
                    )
                if kt == KS and g % 2 == 1:
                    nc.vector.scalar_tensor_tensor(
                        out=junk_v[:],
                        in0=zt[:, KS - 1, :],
                        scalar=1.0,
                        in1=zt[:, KS - 1, :],
                        op0=ALU.mult,
                        op1=ALU.mult,
                        accum_out=sqv[:, g // 2 : g // 2 + 1],
                    )
                if g == G - 1 and kt == KT - 2:
                    for i in range(NG):
                        nc.vector.scalar_tensor_tensor(
                            out=junk_d[:],
                            in0=grams[i][:],
                            scalar=1.0,
                            in1=ident[:],
                            op0=ALU.mult,
                            op1=ALU.mult,
                            accum_out=ssq[:, KS + i : KS + i + 1],
                        )
            if g == 0:
                pv = psum.tile([P, P], BF16, tag="ps", name="pv")
                nc.tensor.transpose(pv[:], vecs[:], ident[:])
                nc.vector.tensor_copy(out=gb[:], in_=pv[:, 0 : 2 * KT])
                pb = psum.tile([P, C], F32, tag="ps", name="pb")
                nc.tensor.matmul(out=pb[:], lhsT=ones[:], rhs=brow[:], start=True, stop=True)
                nc.scalar.copy(out=bias_bc[:], in_=pb[:])

        gw = big.tile([P, 2, C, 4], BF16, tag="big", name="gw", align_bytes=64)

        def w_bank(n):
            c, ct = divmod(n, C // P)
            pw = psum.tile([P, 4, P], BF16, tag="ps", name="pw")
            for t in range(4):
                kt = 4 * c + t
                nc.tensor.transpose(pw[:, t, :], wn[:, ct, kt * P : (kt + 1) * P], ident[:])
            nc.scalar.copy(
                out=gw[:, c, ct * P : (ct + 1) * P, :], in_=pw[:].rearrange("p t n -> p n t")
            )

        for n in range(W_EARLY):
            w_bank(n)

        ssum = const.tile([P, KT], F32, name="ssum")
        nc.vector.tensor_reduce(out=ssum[:], in_=s1[:], axis=AX.X, op=ALU.add)
        sv = const.tile([P, 1], F32, name="sv")
        nc.vector.tensor_reduce(out=sv[:], in_=sqv[:], axis=AX.X, op=ALU.add)
        nc.vector.tensor_reduce(out=ssq[:, 0:KS], in_=sq[:], axis=AX.X, op=ALU.add)
        nc.vector.tensor_tensor(
            out=ssq[:, KS - 1 : KS], in0=ssq[:, KS - 1 : KS], in1=sv[:], op=ALU.add
        )
        m2 = const.tile([P, KT], F32, name="m2")
        nc.vector.scalar_tensor_tensor(
            out=m2[:], in0=ssum[:], scalar=1.0 / (B * B), in1=ssum[:], op0=ALU.mult, op1=ALU.mult
        )
        var = const.tile([P, KT], F32, name="var")
        nc.vector.scalar_tensor_tensor(
            out=var[:], in0=ssq[:], scalar=1.0 / B, in1=m2[:], op0=ALU.mult, op1=ALU.subtract
        )
        ve = const.tile([P, KT], F32, name="ve")
        nc.vector.tensor_scalar(
            out=ve[:], in0=var[:], scalar1=0.0, scalar2=BN_EPS, op0=ALU.max, op1=ALU.add
        )
        sd = const.tile([P, KT], F32, name="sd")
        nc.scalar.activation(out=sd[:], in_=ve[:], func=ACT.Sqrt)
        for n in range(W_EARLY, 2 * C // P):
            w_bank(n)
        mean = const.tile([P, KT], F32, name="mean")
        nc.vector.tensor_scalar(out=mean[:], in0=ssum[:], scalar1=1.0 / B, scalar2=None, op0=ALU.mult)
        rstd = const.tile([P, KT], F32, name="rstd")
        nc.vector.reciprocal(out=rstd[:], in_=sd[:])
        a = const.tile([P, KT], F32, name="a")
        nc.vector.tensor_tensor(out=a[:], in0=gb[:, 0:KT], in1=rstd[:], op=ALU.mult)
        ma = const.tile([P, KT], F32, name="ma")
        nc.vector.tensor_tensor(out=ma[:], in0=mean[:], in1=a[:], op=ALU.mult)
        bb = const.tile([P, KT], F32, name="bb")
        nc.vector.tensor_tensor(out=bb[:], in0=gb[:, KT : 2 * KT], in1=ma[:], op=ALU.subtract)

        ghs = {}
        cds = {}
        scs = {}
        accs = {}
        lts = {}
        negs = {}
        esums = {}
        lnt = {}
        lne = {}
        lnq = {}
        shifts = {}

        def affine(g, kts):
            for kt in kts:
                nc.vector.tensor_scalar(
                    out=zts[g][:, kt, :],
                    in0=zts[g][:, kt, :],
                    scalar1=a[:, kt : kt + 1],
                    scalar2=bb[:, kt : kt + 1],
                    op0=ALU.mult,
                    op1=ALU.add,
                )

        def regroup(u):
            g, h = divmod(u, 2)
            gh = grp.tile([P, 2, UB, 4], BF16, tag="gr", name="gh", align_bytes=64)
            ghs[u] = gh
            if u == 0:
                shares = ((0, 0, UB, "V"), (1, 0, UB, "S"))
            else:
                shares = ((0, 0, UB, "S"), (1, 0, UB - R_TAIL, "S"), (1, UB - R_TAIL, UB, "V"))
            for c, b0, b1, engine in shares:
                dst = gh[:, c, b0:b1, :].rearrange("p (n i) t -> p n t i", i=4)
                src = zts[g][:, 4 * c : 4 * c + 4, h * UB + b0 : h * UB + b1].rearrange(
                    "p t (n i) -> p n t i", i=4
                )
                if engine == "V":
                    nc.vector.tensor_scalar(out=dst, in0=src, scalar1=0.0, scalar2=None, op0=ALU.max)
                else:
                    nc.scalar.activation(out=dst, in_=src, func=ACT.Relu)

        def quant(u):
            cd = cod.tile([P, 2 * UB], U32, tag="cd", name="cd", align_bytes=64)
            sc = cod.tile([P, 2 * UB], U8, tag="sc", name="sc", align_bytes=64)
            cds[u] = cd
            scs[u] = sc
            nc.vector.quantize_mx(
                out=cd[:].bitcast(FP8X4),
                scales=sc[:],
                in_=ghs[u][:].rearrange("p c b t -> p (c b t)"),
            )

        def mx(u):
            for jj in range(JH):
                acc = psum.tile([P, C], F32, tag="ps", name="acc")
                accs[(u, jj)] = acc
                for c in range(2):
                    col = c * UB + jj * P
                    nc.tensor.matmul_mx(
                        out=acc[:],
                        lhsT=cds[u][:, col : col + P].bitcast(FP8X4),
                        lhsT_scale=scs[u][:, col : col + P],
                        rhs=wcodes[:, c * C : (c + 1) * C].bitcast(FP8X4),
                        rhs_scale=wscl[:, c * C : (c + 1) * C],
                        start=(c == 0),
                        stop=(c == 1),
                    )

        def add_bias(u, tiles):
            g, h = divmod(u, 2)
            if h == 0 and tiles[0] == 0:
                lts[g] = big.tile([P, J, C], F32, tag="big", name="lt", align_bytes=64)
                negs[g] = small.tile([P, J], F32, name="neg_m")
                esums[g] = small.tile([P, J], F32, name="esum")
            lt = lts[g]
            for jj in tiles:
                nc.vector.tensor_tensor(
                    out=lt[:, h * JH + jj, :], in0=accs[(u, jj)][:], in1=bias_bc[:], op=ALU.add
                )

        def row_max(u, jj0, jj1):
            g, h = divmod(u, 2)
            nc.vector.tensor_reduce(
                out=negs[g][:, h * JH + jj0 : h * JH + jj1],
                in_=lts[g][:, h * JH + jj0 : h * JH + jj1, :],
                axis=AX.X,
                op=ALU.max,
                negate=True,
            )

        def expsum(u):
            g, h = divmod(u, 2)
            for jj in range(JH):
                j = h * JH + jj
                nc.scalar.activation(
                    out=junk_e[:],
                    in_=lts[g][:, j, :],
                    func=ACT.Exp,
                    bias=negs[g][:, j : j + 1],
                    scale=1.0,
                    accum_out=esums[g][:, j : j + 1],
                )

        def ln_guess(g, j0, j1):
            n = j1 - j0
            r_pos = small.tile([P, J], F32, name="r_pos")
            nc.gpsimd.tensor_tensor(
                out=r_pos[:, 0:n], in0=esums[g][:, j0:j1], in1=pe_pos[:, 0:n], op=ALU.pow
            )
            r_neg = small.tile([P, J], F32, name="r_neg")
            nc.gpsimd.tensor_tensor(
                out=r_neg[:, 0:n], in0=esums[g][:, j0:j1], in1=pe_neg[:, 0:n], op=ALU.pow
            )
            t = small.tile([P, J], F32, name="t")
            lnt[(g, j0)] = t
            nc.gpsimd.tensor_tensor(
                out=t[:, 0:n], in0=r_pos[:, 0:n], in1=r_neg[:, 0:n], op=ALU.subtract
            )
            q = small.tile([P, J], F32, name="q")
            nc.gpsimd.tensor_scalar(
                out=q[:, 0:n],
                in0=t[:, 0:n],
                scalar1=-0.5 * ROOT,
                scalar2=1.0,
                op0=ALU.mult,
                op1=ALU.add,
            )
            q2 = small.tile([P, J], F32, name="q2")
            lnq[(g, j0)] = q2
            nc.gpsimd.tensor_tensor(
                out=q2[:, 0:n], in0=q[:, 0:n], in1=negs[g][:, j0:j1], op=ALU.add
            )

        def ln_step(g, j0, j1):
            n = j1 - j0
            e = small.tile([P, J], F32, name="e")
            nc.scalar.activation(
                out=e[:, 0:n], in_=lnt[(g, j0)][:, 0:n], func=ACT.Exp, scale=-0.5 * ROOT
            )
            w = small.tile([P, J], F32, name="w")
            nc.gpsimd.tensor_tensor(
                out=w[:, 0:n], in0=esums[g][:, j0:j1], in1=e[:, 0:n], op=ALU.mult
            )
            neg_c = small.tile([P, J], F32, name="neg_c")
            shifts[(g, j0)] = neg_c
            nc.gpsimd.tensor_tensor(
                out=neg_c[:, 0:n], in0=lnq[(g, j0)][:, 0:n], in1=w[:, 0:n], op=ALU.subtract
            )

        def ln_table(g, j0, j1):
            y = small.tile([P, J], F32, name="y")
            lne[(g, j0)] = y
            nc.scalar.activation(out=y[:, 0 : j1 - j0], in_=esums[g][:, j0:j1], func=ACT.Ln)

        def ln_table_shift(g, j0, j1):
            n = j1 - j0
            neg_c = small.tile([P, J], F32, name="neg_c")
            shifts[(g, j0)] = neg_c
            nc.vector.tensor_tensor(
                out=neg_c[:, 0:n], in0=negs[g][:, j0:j1], in1=lne[(g, j0)][:, 0:n], op=ALU.subtract
            )

        def subtract_store(g, h, key, engines, per_store):
            lt = lts[g]
            for jj in range(JH):
                j = h * JH + jj
                shift = shifts[key][:, j - key[1] : j - key[1] + 1]
                engine = engines[jj]
                if engine == "V":
                    nc.vector.tensor_scalar(
                        out=lt[:, j, :], in0=lt[:, j, :], scalar1=shift, scalar2=None, op0=ALU.add
                    )
                elif engine == "G":
                    nc.gpsimd.tensor_scalar(
                        out=lt[:, j, :],
                        in0=lt[:, j, :],
                        scalar1=1.0,
                        scalar2=shift,
                        op0=ALU.mult,
                        op1=ALU.add,
                    )
                else:
                    nc.scalar.activation(
                        out=lt[:, j, :], in_=lt[:, j, :], func=ACT.Identity, bias=shift, scale=1.0
                    )
                if jj % per_store == per_store - 1:
                    rows = out[(2 * g + h) * UB : (2 * g + h + 1) * UB, :]
                    nc.sync.dma_start(
                        out=rows.rearrange("(p j) c -> p j c", j=JH)[:, jj + 1 - per_store : jj + 1, :],
                        in_=lt[:, j + 1 - per_store : j + 1, :],
                    )

        affine(0, range(KT))
        regroup(0)
        regroup(1)
        nc.vector.quantize_mx(
            out=wcodes[:].bitcast(FP8X4),
            scales=wscl[:],
            in_=gw[:].rearrange("p c n t -> p (c n t)"),
        )
        quant(0)
        mx(0)
        affine(1, range(KT))
        for v in range(U + 1):
            if v + 1 < U:
                quant(v + 1)
                mx(v + 1)
            if v + 2 < U:
                regroup(v + 2)
            if v < U - 1:
                add_bias(v, range(JH))
            if v == U - 1:
                for jj in range(JH):
                    add_bias(v, range(jj, jj + 1))
                    if jj >= 1:
                        row_max(v, jj - 1, jj)
                row_max(v, JH - 1, JH)
            if v >= 1:
                expsum(v - 1)
            gf, odd = divmod(v - 2, 2)
            if v >= 2 and odd == 0 and gf < G - 1:
                ln_guess(gf, 0, J)
            if v >= 3 and odd == 1:
                ln_step(gf, 0, J)
            if v == U:
                ln_table(G - 1, 0, J)
            if v + 4 < U:
                half = range(0, 4) if v % 2 == 0 else range(4, KT)
                affine((v + 4) // 2, half)
            if v < U - 1:
                row_max(v, 0, JH)
            if v >= 3 and odd == 1:
                subtract_store(gf, 0, (gf, 0), "GGGG" if v < U - 2 else "SSSS", JH)
            if v >= 4 and odd == 0:
                subtract_store(gf - 1, 1, (gf - 1, 0), "GGGG" if v < U - 2 else "VVVV", JH)
            if v == U:
                ln_table_shift(G - 1, 0, J)
                subtract_store(G - 1, 0, (G - 1, 0), "VVVV", JH)
                subtract_store(G - 1, 1, (G - 1, 0), "SSVV", JH // 2)
